import numpy as np
import ml_dtypes


def mxq(x, axis, fmt="e4m3"):
    dtype, down = {"e4m3": (ml_dtypes.float8_e4m3fn, 7), "e5m2": (ml_dtypes.float8_e5m2, 14)}[fmt]
    v = np.moveaxis(np.asarray(x, np.float32).astype(ml_dtypes.bfloat16).astype(np.float64), axis, -1)
    blocks = v.reshape(v.shape[:-1] + (-1, 32))
    amax = np.abs(blocks).max(-1, keepdims=True)
    byte = np.maximum(np.where(amax > 0, np.frexp(amax)[1] - 1 + 127, 0) - down, 1)
    scale = np.exp2(byte - 127.0)
    codes = (blocks / scale).astype(np.float32).astype(dtype).astype(np.float64)
    return np.moveaxis((codes * scale).reshape(v.shape), -1, axis)


WIDE = False


def mx_kscale(k):
    if not WIDE:
        return np.ones(k)
    levels = np.array([10, -10, 5, -5, 0])
    a = np.random.permutation(np.resize(levels, k // 512 * 4)).reshape(k // 512, 4)
    idx = np.arange(k)
    return np.exp2(a[idx // 512, idx % 128 // 32])


BF16 = ml_dtypes.bfloat16


def bf(x):
    return np.asarray(x, np.float32).astype(BF16)


def f64(x):
    return np.asarray(x).astype(np.float64)


B, T, C, H, KV, D = 2, 256, 2048, 16, 4, 128
EPS = 1e-5
THETA = 10000.0


def rmsnorm(h, w):
    var = np.mean(np.square(h), axis=-1, keepdims=True)
    return h * (1.0 / np.sqrt(var + EPS)) * w


def rope(h, cos, sin):
    hr = h.reshape(*h.shape[:-1], D // 2, 2)
    a, b = hr[..., 0], hr[..., 1]
    c = cos[None, :, None, :]
    s = sin[None, :, None, :]
    return np.stack([a * c - b * s, a * s + b * c], axis=-1).reshape(h.shape)


def setup_inputs():
    s = mx_kscale(C)
    w_scale = 1.0 / np.sqrt(C)
    inv_freq = 1.0 / (THETA ** (np.arange(0, D, 2) / D))
    angles = np.arange(T)[:, None] * inv_freq[None, :]
    return {"x": bf(np.random.standard_normal((B, T, C)) * s),
            "Wq": bf(np.random.standard_normal((C, H * D)) * w_scale / s[:, None]),
            "bq": bf(np.random.standard_normal(H * D) * 0.1),
            "Wk": bf(np.random.standard_normal((C, KV * D)) * w_scale / s[:, None]),
            "bk": bf(np.random.standard_normal(KV * D) * 0.1),
            "Wv": bf(np.random.standard_normal((C, KV * D)) * w_scale / s[:, None]),
            "bv": bf(np.random.standard_normal(KV * D) * 0.1),
            "qn_w": bf(1.0 + 0.1 * np.random.standard_normal(D)),
            "kn_w": bf(1.0 + 0.1 * np.random.standard_normal(D)),
            "freqs_cos": bf(np.cos(angles)),
            "freqs_sin": bf(np.sin(angles))}


def reference(x, Wq, bq, Wk, bk, Wv, bv, qn_w, kn_w, freqs_cos, freqs_sin):
    xq = mxq(f64(x), 2, "e4m3")
    q = ((xq @ mxq(f64(Wq), 0, "e4m3")) + f64(bq)).reshape(B, T, H, D)
    k = ((xq @ mxq(f64(Wk), 0, "e4m3")) + f64(bk)).reshape(B, T, KV, D)
    v = ((xq @ mxq(f64(Wv), 0, "e4m3")) + f64(bv)).reshape(B, T, KV, D)
    q = rmsnorm(q, f64(qn_w))
    k = rmsnorm(k, f64(kn_w))
    q = rope(q, f64(freqs_cos), f64(freqs_sin))
    k = rope(k, f64(freqs_cos), f64(freqs_sin))
    return q, k, v

@@ -1,0 +1,340 @@
+from contextlib import ExitStack
+
+import concourse.mybir as mybir
+from concourse.masks import make_identity
+
+F32 = mybir.dt.float32
+BF16 = mybir.dt.bfloat16
+U32 = mybir.dt.uint32
+U8 = mybir.dt.uint8
+FP8X4 = mybir.dt.float8_e4m3fn_x4
+ALU = mybir.AluOpType
+ACT = mybir.ActivationFunctionType
+
+BATCH, SEQ, WIDTH = 2, 256, 2048
+Q_HEADS, KV_HEADS, HEAD = 16, 4, 128
+EPS = 1e-5
+
+P = 128
+PACK = 4
+K_PASS = P * PACK
+PASSES = WIDTH // K_PASS
+TOKENS = BATCH * SEQ
+TOKEN_TILES = TOKENS // P
+SEQ_TILES = SEQ // P
+CHUNK = 512
+CHUNK_HEADS = CHUNK // HEAD
+Q_CHUNKS = Q_HEADS // CHUNK_HEADS
+K_CHUNK = Q_CHUNKS
+V_CHUNK = Q_CHUNKS + 1
+CHUNKS = Q_CHUNKS + 2
+W_TILES = CHUNKS * PASSES
+ROPE_HEADS = Q_HEADS + KV_HEADS
+UNIT_HEADS = 2
+ROPE_UNITS = ROPE_HEADS // UNIT_HEADS
+RAW_BUFS = 8
+VECTOR_COLS = 320
+GAIN_COL = ROPE_HEADS
+
+FLOPS = 2 * TOKENS * WIDTH * (Q_HEADS + 2 * KV_HEADS) * HEAD
+
+
+def tile_llamacausalselfattention_pa_kernel(
+    tc, x, Wq, bq, Wk, bk, Wv, bv, qn_w, kn_w, freqs_cos, freqs_sin, out_0, out_1, out_2
+):
+    nc = tc.nc
+    with ExitStack() as pools:
+        const = pools.enter_context(tc.tile_pool(name="const", bufs=1))
+        xpool = pools.enter_context(tc.tile_pool(name="xpool", bufs=1))
+        wraw = pools.enter_context(tc.tile_pool(name="wraw", bufs=RAW_BUFS))
+        wgrp = pools.enter_context(tc.tile_pool(name="wgrp", bufs=4))
+        wmx = pools.enter_context(tc.tile_pool(name="wmx", bufs=1))
+        work = pools.enter_context(tc.tile_pool(name="work", bufs=4))
+        stats = pools.enter_context(tc.tile_pool(name="stats", bufs=4))
+        outs = pools.enter_context(tc.tile_pool(name="outs", bufs=3))
+        psum_acc = pools.enter_context(tc.psum_pool(name="psum_acc", bufs=4))
+        psum_back = pools.enter_context(tc.psum_pool(name="psum_back", bufs=3))
+        psum_ss = pools.enter_context(tc.psum_pool(name="psum_ss", bufs=1))
+
+        rows_bf = const.tile([P, P], BF16)
+        nc.vector.memset(rows_bf[:], 0.0)
+        nc.scalar.dma_start(out=rows_bf[0:Q_HEADS, :], in_=bq.rearrange("(h d) -> h d", d=HEAD))
+        nc.scalar.dma_start(
+            out=rows_bf[Q_HEADS:ROPE_HEADS, :], in_=bk.rearrange("(h d) -> h d", d=HEAD)
+        )
+        nc.scalar.dma_start(
+            out=rows_bf[GAIN_COL : GAIN_COL + 1, :], in_=qn_w.rearrange("(o d) -> o d", o=1)
+        )
+        nc.scalar.dma_start(
+            out=rows_bf[GAIN_COL + 1 : GAIN_COL + 2, :], in_=kn_w.rearrange("(o d) -> o d", o=1)
+        )
+        cos_sin = const.tile([P, 2, SEQ_TILES, HEAD // 2], BF16)
+        nc.scalar.dma_start(out=cos_sin[:, 0, :, :], in_=freqs_cos.rearrange("(a p) j -> p a j", p=P))
+        nc.scalar.dma_start(out=cos_sin[:, 1, :, :], in_=freqs_sin.rearrange("(a p) j -> p a j", p=P))
+        bv_all = const.tile([P, CHUNK], BF16)
+        nc.scalar.dma_start(out=bv_all[:], in_=bv.partition_broadcast(P))
+
+        x_rows = x.flatten_outer_dims()
+        x_raw = xpool.tile([P, TOKEN_TILES, WIDTH], BF16)
+        for m in range(TOKEN_TILES):
+            nc.sync.dma_start(out=x_raw[:, m, :], in_=x_rows[m * P : (m + 1) * P, :])
+
+        def weight_columns(g):
+            if g < Q_CHUNKS:
+                return Wq[:, g * CHUNK : (g + 1) * CHUNK]
+            return Wk if g == K_CHUNK else Wv
+
+        raw_tiles = {}
+        grouped_tiles = {}
+
+        def load_weight_tile(j):
+            g, c = divmod(j, PASSES)
+            raw = wraw.tile([P, PACK, CHUNK], BF16)
+            nc.sync.dma_start(
+                out=raw[:],
+                in_=weight_columns(g).rearrange("(c p t) n -> c p t n", p=P, t=PACK)[c],
+            )
+            raw_tiles[j] = raw
+
+        for j in range(RAW_BUFS):
+            load_weight_tile(j)
+
+        ident = const.tile([P, P], F32)
+        make_identity(nc, ident[:])
+        swap = const.tile([P, P], F32)
+        ident_pairs = ident[:].rearrange("p (j two) -> p j two", two=2)
+        swap_pairs = swap[:].rearrange("p (j two) -> p j two", two=2)
+        nc.vector.tensor_copy(out=swap_pairs[:, :, 0], in_=ident_pairs[:, :, 1])
+        nc.vector.tensor_copy(out=swap_pairs[:, :, 1], in_=ident_pairs[:, :, 0])
+        ones = const.tile([P, 2], F32)
+        nc.vector.memset(ones[:], 1.0)
+
+        rows_f32 = const.tile([P, P], F32)
+        nc.vector.tensor_copy(out=rows_f32[:], in_=rows_bf[:])
+        rows_ps = psum_back.tile([P, P], F32, tag="back")
+        nc.tensor.transpose(rows_ps[:], rows_f32[:], ident[:])
+        per_feature = const.tile([P, P], F32)
+        nc.vector.tensor_copy(out=per_feature[:], in_=rows_ps[:])
+
+        spread = const.tile([P, 2, SEQ_TILES, HEAD], F32)
+        cos_pairs = spread[:, 0, :, :].rearrange("p a (j two) -> p a j two", two=2)
+        sin_pairs = spread[:, 1, :, :].rearrange("p a (j two) -> p a j two", two=2)
+        nc.vector.tensor_copy(
+            out=cos_pairs,
+            in_=cos_sin[:, 0, :, :].unsqueeze(3).to_broadcast([P, SEQ_TILES, HEAD // 2, 2]),
+        )
+        nc.vector.tensor_copy(out=sin_pairs[:, :, :, 0], in_=cos_sin[:, 1, :, :])
+        nc.vector.tensor_scalar_mul(out=sin_pairs[:, :, :, 1], in0=cos_sin[:, 1, :, :], scalar1=-1.0)
+        spread_ps = psum_back.tile([P, 2, SEQ_TILES, P], F32, tag="back")
+        for s in range(2):
+            for a in range(SEQ_TILES):
+                nc.tensor.transpose(spread_ps[:, s, a, :], spread[:, s, a, :], ident[:])
+        tables = const.tile([P, 2, 2, SEQ], F32)
+        for w in range(2):
+            nc.scalar.activation(
+                out=tables[:, w, :, :],
+                in_=spread_ps[:].rearrange("p s a t -> p s (a t)"),
+                func=ACT.Copy,
+                scale=per_feature[:, GAIN_COL + w : GAIN_COL + w + 1],
+            )
+
+        x_grouped = xpool.tile([P, PASSES, TOKENS * PACK], BF16, align_bytes=64)
+        x_codes = xpool.tile([P, PASSES, TOKENS], U32, align_bytes=64)
+        x_scales = xpool.tile([P, PASSES, TOKENS], U8, align_bytes=64)
+        x_grouped_words = x_grouped[:].bitcast(F32).rearrange("p c (r u) -> p c r u", u=2)
+        for m in range(TOKEN_TILES):
+            x_words = x_raw[:, m, :].bitcast(F32).rearrange("p (c w u) -> p c u w", c=PASSES, u=2)
+            for half in range(2):
+                turned = psum_acc.tile([P, 2, 2, P], F32, tag="acc")
+                for c2 in range(2):
+                    for u in range(2):
+                        nc.tensor.transpose(turned[:, c2, u, :], x_words[:, 2 * half + c2, u, :], ident[:])
+                copy_out = nc.vector.tensor_copy if half == 0 else nc.scalar.copy
+                copy_out(
+                    out=x_grouped_words[:, 2 * half : 2 * half + 2, m * P : (m + 1) * P, :],
+                    in_=turned[:].rearrange("p c u r -> p c r u"),
+                )
+        for c in range(PASSES):
+            nc.vector.quantize_mx(
+                out=x_codes[:, c, :].bitcast(FP8X4), scales=x_scales[:, c, :], in_=x_grouped[:, c, :]
+            )
+
+        w_codes = [wmx.tile([P, PASSES, CHUNK], U32, align_bytes=64, name="w_codes%d" % g) for g in range(CHUNKS)]
+        w_scales = [wmx.tile([P, PASSES, CHUNK], U8, align_bytes=64, name="w_scales%d" % g) for g in range(CHUNKS)]
+
+        def regroup_weight_tile(j):
+            raw = raw_tiles[j]
+            grouped = wgrp.tile([P, CHUNK, PACK], BF16, align_bytes=64)
+            nc.vector.tensor_copy(
+                out=grouped[:, :VECTOR_COLS, :].rearrange("p (n i) t -> p n t i", i=4),
+                in_=raw[:, :, :VECTOR_COLS].rearrange("p t (n i) -> p n t i", i=4),
+            )
+            nc.scalar.copy(
+                out=grouped[:, VECTOR_COLS:, :].rearrange("p (n i) t -> p n t i", i=4),
+                in_=raw[:, :, VECTOR_COLS:].rearrange("p t (n i) -> p n t i", i=4),
+            )
+            grouped_tiles[j] = grouped
+
+        def quantise_weight_tile(j):
+            g, c = divmod(j, PASSES)
+            nc.vector.quantize_mx(
+                out=w_codes[g][:, c, :].bitcast(FP8X4),
+                scales=w_scales[g][:, c, :],
+                in_=grouped_tiles[j][:].rearrange("p n t -> p (n t)"),
+            )
+
+        def prepare(j):
+            if j < W_TILES:
+                regroup_weight_tile(j)
+                if j + RAW_BUFS < W_TILES:
+                    load_weight_tile(j + RAW_BUFS)
+            if 1 <= j <= W_TILES:
+                quantise_weight_tile(j - 1)
+
+        acc_tiles = {}
+        rotated = {}
+        back_tiles = {}
+        rstd_tiles = {}
+        out_tiles = {}
+        sum_squares = psum_ss.tile([P, ROPE_HEADS, TOKEN_TILES, 2], F32)
+
+        def unit_heads(i):
+            return range(i * UNIT_HEADS, (i + 1) * UNIT_HEADS)
+
+        def project(i):
+            for n in unit_heads(i):
+                g, local = divmod(n, CHUNK_HEADS)
+                cols = slice(local * HEAD, (local + 1) * HEAD)
+                acc = psum_acc.tile([P, TOKENS], F32, tag="acc")
+                for c in range(PASSES):
+                    nc.tensor.matmul_mx(
+                        out=acc[:],
+                        lhsT=w_codes[g][:, c, cols].bitcast(FP8X4),
+                        lhsT_scale=w_scales[g][:, c, cols],
+                        rhs=x_codes[:, c, :].bitcast(FP8X4),
+                        rhs_scale=x_scales[:, c, :],
+                        start=(c == 0),
+                        stop=(c == PASSES - 1),
+                    )
+                acc_tiles[n] = acc
+
+        def rotate_terms(i):
+            for n in unit_heads(i):
+                acc = acc_tiles[n]
+                bias = per_feature[:, n : n + 1]
+                w = 0 if n < Q_HEADS else 1
+                by_cos = work.tile([P, TOKENS], F32)
+                by_sin = work.tile([P, TOKENS], F32)
+                for s, term in enumerate((by_cos, by_sin)):
+                    nc.vector.scalar_tensor_tensor(
+                        out=term[:].rearrange("p (b t) -> p b t", b=BATCH),
+                        in0=acc[:].rearrange("p (b t) -> p b t", b=BATCH),
+                        scalar=bias,
+                        in1=tables[:, w, s, :].unsqueeze(1).to_broadcast([P, BATCH, SEQ]),
+                        op0=ALU.add,
+                        op1=ALU.mult,
+                    )
+                squares = work.tile([P, TOKENS], F32)
+                nc.scalar.activation(out=squares[:], in_=acc[:], func=ACT.Square, bias=bias, scale=1.0)
+                rotated[n] = (by_cos, by_sin, squares)
+
+        def turn_back(i):
+            for n in unit_heads(i):
+                by_cos, by_sin, squares = rotated[n]
+                back = psum_back.tile([P, TOKEN_TILES, HEAD], F32, tag="back")
+                for m in range(TOKEN_TILES):
+                    tokens = slice(m * P, (m + 1) * P)
+                    nc.tensor.matmul(
+                        out=back[:, m, :], lhsT=by_cos[:, tokens], rhs=ident[:],
+                        is_transpose=True, start=True, stop=False,
+                    )
+                    nc.tensor.matmul(
+                        out=back[:, m, :], lhsT=by_sin[:, tokens], rhs=swap[:],
+                        is_transpose=True, start=False, stop=True,
+                    )
+                back_tiles[n] = back
+            for n in unit_heads(i):
+                squares = rotated[n][2]
+                for m in range(TOKEN_TILES):
+                    nc.tensor.matmul(
+                        out=sum_squares[:, n, m, :], lhsT=squares[:, m * P : (m + 1) * P], rhs=ones[:],
+                        start=True, stop=True,
+                    )
+
+        def norm_factors(i):
+            first = i * UNIT_HEADS
+            rms = stats.tile([P, UNIT_HEADS, TOKEN_TILES], F32)
+            nc.scalar.activation(
+                out=rms[:], in_=sum_squares[:, first : first + UNIT_HEADS, :, 0],
+                func=ACT.Sqrt, bias=EPS, scale=1.0 / HEAD,
+            )
+            rstd = stats.tile([P, UNIT_HEADS, TOKEN_TILES], F32)
+            nc.vector.reciprocal(out=rstd[:], in_=rms[:])
+            rstd_tiles[i] = rstd
+
+        def finish(i):
+            g = (i * UNIT_HEADS) // CHUNK_HEADS
+            if g not in out_tiles:
+                out_tiles[g] = outs.tile([P, TOKEN_TILES, CHUNK], F32, name="result")
+            result = out_tiles[g]
+            for h, n in enumerate(unit_heads(i)):
+                local = n % CHUNK_HEADS
+                for m in range(TOKEN_TILES):
+                    nc.scalar.activation(
+                        out=result[:, m, local * HEAD : (local + 1) * HEAD],
+                        in_=back_tiles[n][:, m, :],
+                        func=ACT.Copy,
+                        scale=rstd_tiles[i][:, h, m : m + 1],
+                    )
+            if (i + 1) * UNIT_HEADS % CHUNK_HEADS == 0:
+                if g < Q_CHUNKS:
+                    dest = out_0.rearrange("b t h d -> (b t) (h d)")[:, g * CHUNK : (g + 1) * CHUNK]
+                else:
+                    dest = out_1.rearrange("b t h d -> (b t) (h d)")
+                nc.scalar.dma_start(out=dest.rearrange("(m p) n -> p m n", p=P), in_=result[:])
+
+        def project_v(m):
+            acc = psum_acc.tile([P, CHUNK], F32, tag="acc")
+            tokens = slice(m * P, (m + 1) * P)
+            for c in range(PASSES):
+                nc.tensor.matmul_mx(
+                    out=acc[:],
+                    lhsT=x_codes[:, c, tokens].bitcast(FP8X4),
+                    lhsT_scale=x_scales[:, c, tokens],
+                    rhs=w_codes[V_CHUNK][:, c, :].bitcast(FP8X4),
+                    rhs_scale=w_scales[V_CHUNK][:, c, :],
+                    start=(c == 0),
+                    stop=(c == PASSES - 1),
+                )
+            return acc
+
+        def finish_v(m, acc):
+            v_rows = outs.tile([P, CHUNK], F32)
+            nc.vector.tensor_tensor(out=v_rows[:], in0=acc[:], in1=bv_all[:], op=ALU.add)
+            nc.sync.dma_start(
+                out=out_2.rearrange("b t h d -> (b t) (h d)")[m * P : (m + 1) * P, :], in_=v_rows[:]
+            )
+
+        LEAD = PASSES + 3
+        for j in range(PASSES + 1):
+            prepare(j)
+        project(0)
+        for j in range(PASSES + 1, LEAD):
+            prepare(j)
+        for i in range(ROPE_UNITS):
+            if i + 1 < ROPE_UNITS:
+                project(i + 1)
+            else:
+                v_acc = [project_v(m) for m in range(UNIT_HEADS)]
+            if i >= 1:
+                norm_factors(i - 1)
+                finish(i - 1)
+            rotate_terms(i)
+            turn_back(i)
+            prepare(LEAD + 2 * i)
+            prepare(LEAD + 2 * i + 1)
+        v_acc.extend([project_v(m) for m in range(UNIT_HEADS, TOKEN_TILES)])
+        norm_factors(ROPE_UNITS - 1)
+        finish(ROPE_UNITS - 1)
+        for m in range(TOKEN_TILES):
+            finish_v(m, v_acc[m])

@@ -55,6 +55,7 @@ def tile_llamacausalselfattention_pa_kernel(
         psum_acc = pools.enter_context(tc.psum_pool(name="psum_acc", bufs=4))
         psum_back = pools.enter_context(tc.psum_pool(name="psum_back", bufs=3))
         psum_ss = pools.enter_context(tc.psum_pool(name="psum_ss", bufs=1))
+        pools.enter_context(tc.manual_schedule())
 
         rows_bf = const.tile([P, P], BF16)
         nc.vector.memset(rows_bf[:], 0.0)
@@ -74,10 +75,10 @@ def tile_llamacausalselfattention_pa_kernel(
         bv_all = const.tile([P, CHUNK], BF16)
         nc.scalar.dma_start(out=bv_all[:], in_=bv.partition_broadcast(P))
 
-        x_rows = x.flatten_outer_dims()
-        x_raw = xpool.tile([P, TOKEN_TILES, WIDTH], BF16)
-        for m in range(TOKEN_TILES):
-            nc.sync.dma_start(out=x_raw[:, m, :], in_=x_rows[m * P : (m + 1) * P, :])
+        x_blocks = x.flatten_outer_dims().rearrange("(m p) k -> p m k", p=P)
+        x_raw = xpool.tile([P, PASSES, TOKEN_TILES, K_PASS], BF16)
+        for c in range(PASSES):
+            nc.sync.dma_start(out=x_raw[:, c, :, :], in_=x_blocks[:, :, c * K_PASS : (c + 1) * K_PASS])
 
         def weight_columns(g):
             if g < Q_CHUNKS:
@@ -111,11 +112,6 @@ def tile_llamacausalselfattention_pa_kernel(
 
         rows_f32 = const.tile([P, P], F32)
         nc.vector.tensor_copy(out=rows_f32[:], in_=rows_bf[:])
-        rows_ps = psum_back.tile([P, P], F32, tag="back")
-        nc.tensor.transpose(rows_ps[:], rows_f32[:], ident[:])
-        per_feature = const.tile([P, P], F32)
-        nc.vector.tensor_copy(out=per_feature[:], in_=rows_ps[:])
-
         spread = const.tile([P, 2, SEQ_TILES, HEAD], F32)
         cos_pairs = spread[:, 0, :, :].rearrange("p a (j two) -> p a j two", two=2)
         sin_pairs = spread[:, 1, :, :].rearrange("p a (j two) -> p a j two", two=2)
@@ -125,39 +121,51 @@ def tile_llamacausalselfattention_pa_kernel(
         )
         nc.vector.tensor_copy(out=sin_pairs[:, :, :, 0], in_=cos_sin[:, 1, :, :])
         nc.vector.tensor_scalar_mul(out=sin_pairs[:, :, :, 1], in0=cos_sin[:, 1, :, :], scalar1=-1.0)
-        spread_ps = psum_back.tile([P, 2, SEQ_TILES, P], F32, tag="back")
-        for s in range(2):
-            for a in range(SEQ_TILES):
-                nc.tensor.transpose(spread_ps[:, s, a, :], spread[:, s, a, :], ident[:])
+        per_feature = const.tile([P, P], F32)
         tables = const.tile([P, 2, 2, SEQ], F32)
-        for w in range(2):
-            nc.scalar.activation(
-                out=tables[:, w, :, :],
-                in_=spread_ps[:].rearrange("p s a t -> p s (a t)"),
-                func=ACT.Copy,
-                scale=per_feature[:, GAIN_COL + w : GAIN_COL + w + 1],
-            )
+
+        def build_tables():
+            rows_ps = psum_back.tile([P, P], F32, tag="back")
+            nc.tensor.transpose(rows_ps[:], rows_f32[:], ident[:])
+            nc.scalar.copy(out=per_feature[:], in_=rows_ps[:])
+            spread_ps = psum_back.tile([P, 2, SEQ_TILES, P], F32, tag="back")
+            for s in range(2):
+                for a in range(SEQ_TILES):
+                    nc.tensor.transpose(spread_ps[:, s, a, :], spread[:, s, a, :], ident[:])
+            for w in range(2):
+                nc.scalar.activation(
+                    out=tables[:, w, :, :],
+                    in_=spread_ps[:].rearrange("p s a t -> p s (a t)"),
+                    func=ACT.Copy,
+                    scale=per_feature[:, GAIN_COL + w : GAIN_COL + w + 1],
+                )
 
         x_grouped = xpool.tile([P, PASSES, TOKENS * PACK], BF16, align_bytes=64)
         x_codes = xpool.tile([P, PASSES, TOKENS], U32, align_bytes=64)
         x_scales = xpool.tile([P, PASSES, TOKENS], U8, align_bytes=64)
-        x_grouped_words = x_grouped[:].bitcast(F32).rearrange("p c (r u) -> p c r u", u=2)
-        for m in range(TOKEN_TILES):
-            x_words = x_raw[:, m, :].bitcast(F32).rearrange("p (c w u) -> p c u w", c=PASSES, u=2)
-            for half in range(2):
-                turned = psum_acc.tile([P, 2, 2, P], F32, tag="acc")
-                for c2 in range(2):
-                    for u in range(2):
-                        nc.tensor.transpose(turned[:, c2, u, :], x_words[:, 2 * half + c2, u, :], ident[:])
-                copy_out = nc.vector.tensor_copy if half == 0 else nc.scalar.copy
-                copy_out(
-                    out=x_grouped_words[:, 2 * half : 2 * half + 2, m * P : (m + 1) * P, :],
-                    in_=turned[:].rearrange("p c u r -> p c r u"),
-                )
-        for c in range(PASSES):
+        x_grouped_words = x_grouped[:].bitcast(F32).rearrange("p c (m r u) -> p c m r u", m=TOKEN_TILES, u=2)
+
+        def quantise_x(c):
             nc.vector.quantize_mx(
                 out=x_codes[:, c, :].bitcast(FP8X4), scales=x_scales[:, c, :], in_=x_grouped[:, c, :]
             )
+
+        for c in range(PASSES):
+            x_words = x_raw[:, c, :, :].bitcast(F32).rearrange("p m (w u) -> p m u w", u=2)
+            for half, copy_out in enumerate((nc.vector.tensor_copy, nc.scalar.copy)):
+                turned = psum_acc.tile([P, 2, 2, P], F32, tag="acc")
+                for m2 in range(2):
+                    for u in range(2):
+                        nc.tensor.transpose(turned[:, m2, u, :], x_words[:, 2 * half + m2, u, :], ident[:])
+                copy_out(
+                    out=x_grouped_words[:, c, 2 * half : 2 * half + 2, :, :],
+                    in_=turned[:].rearrange("p m u r -> p m r u"),
+                )
+            if c == 0:
+                build_tables()
+            else:
+                quantise_x(c - 1)
+        quantise_x(PASSES - 1)
 
         w_codes = [wmx.tile([P, PASSES, CHUNK], U32, align_bytes=64, name="w_codes%d" % g) for g in range(CHUNKS)]
         w_scales = [wmx.tile([P, PASSES, CHUNK], U8, align_bytes=64, name="w_scales%d" % g) for g in range(CHUNKS)]
@@ -193,6 +201,7 @@ def tile_llamacausalselfattention_pa_kernel(
 
         acc_tiles = {}
         rotated = {}
+        squared = {}
         back_tiles = {}
         rstd_tiles = {}
         out_tiles = {}
@@ -234,13 +243,19 @@ def tile_llamacausalselfattention_pa_kernel(
                         op0=ALU.add,
                         op1=ALU.mult,
                     )
+                rotated[n] = (by_cos, by_sin)
+
+        def square(i):
+            for n in unit_heads(i):
                 squares = work.tile([P, TOKENS], F32)
-                nc.scalar.activation(out=squares[:], in_=acc[:], func=ACT.Square, bias=bias, scale=1.0)
-                rotated[n] = (by_cos, by_sin, squares)
+                nc.scalar.activation(
+                    out=squares[:], in_=acc_tiles[n][:], func=ACT.Square, bias=per_feature[:, n : n + 1], scale=1.0
+                )
+                squared[n] = squares
 
         def turn_back(i):
             for n in unit_heads(i):
-                by_cos, by_sin, squares = rotated[n]
+                by_cos, by_sin = rotated[n]
                 back = psum_back.tile([P, TOKEN_TILES, HEAD], F32, tag="back")
                 for m in range(TOKEN_TILES):
                     tokens = slice(m * P, (m + 1) * P)
@@ -253,8 +268,10 @@ def tile_llamacausalselfattention_pa_kernel(
                         is_transpose=True, start=False, stop=True,
                     )
                 back_tiles[n] = back
+
+        def sum_over_features(i):
             for n in unit_heads(i):
-                squares = rotated[n][2]
+                squares = squared[n]
                 for m in range(TOKEN_TILES):
                     nc.tensor.matmul(
                         out=sum_squares[:, n, m, :], lhsT=squares[:, m * P : (m + 1) * P], rhs=ones[:],
@@ -319,6 +336,7 @@ def tile_llamacausalselfattention_pa_kernel(
         for j in range(PASSES + 1):
             prepare(j)
         project(0)
+        square(0)
         for j in range(PASSES + 1, LEAD):
             prepare(j)
         for i in range(ROPE_UNITS):
@@ -327,14 +345,16 @@ def tile_llamacausalselfattention_pa_kernel(
             else:
                 v_acc = [project_v(m) for m in range(UNIT_HEADS)]
             if i >= 1:
-                norm_factors(i - 1)
                 finish(i - 1)
             rotate_terms(i)
+            sum_over_features(i)
             turn_back(i)
             prepare(LEAD + 2 * i)
             prepare(LEAD + 2 * i + 1)
+            norm_factors(i)
+            if i + 1 < ROPE_UNITS:
+                square(i + 1)
         v_acc.extend([project_v(m) for m in range(UNIT_HEADS, TOKEN_TILES)])
-        norm_factors(ROPE_UNITS - 1)
         finish(ROPE_UNITS - 1)
         for m in range(TOKEN_TILES):
             finish_v(m, v_acc[m])

@@ -34,6 +34,7 @@ UNIT_HEADS = 2
 ROPE_UNITS = ROPE_HEADS // UNIT_HEADS
 RAW_BUFS = 8
 VECTOR_COLS = 320
+ONES_COLS = 64
 GAIN_COL = ROPE_HEADS
 
 FLOPS = 2 * TOKENS * WIDTH * (Q_HEADS + 2 * KV_HEADS) * HEAD
@@ -107,7 +108,7 @@ def tile_llamacausalselfattention_pa_kernel(
         swap_pairs = swap[:].rearrange("p (j two) -> p j two", two=2)
         nc.vector.tensor_copy(out=swap_pairs[:, :, 0], in_=ident_pairs[:, :, 1])
         nc.vector.tensor_copy(out=swap_pairs[:, :, 1], in_=ident_pairs[:, :, 0])
-        ones = const.tile([P, 2], F32)
+        ones = const.tile([P, ONES_COLS], F32)
         nc.vector.memset(ones[:], 1.0)
 
         rows_f32 = const.tile([P, P], F32)
@@ -205,7 +206,7 @@ def tile_llamacausalselfattention_pa_kernel(
         back_tiles = {}
         rstd_tiles = {}
         out_tiles = {}
-        sum_squares = psum_ss.tile([P, ROPE_HEADS, TOKEN_TILES, 2], F32)
+        sums_tiles = {}
 
         def unit_heads(i):
             return range(i * UNIT_HEADS, (i + 1) * UNIT_HEADS)
@@ -270,19 +271,20 @@ def tile_llamacausalselfattention_pa_kernel(
                 back_tiles[n] = back
 
         def sum_over_features(i):
-            for n in unit_heads(i):
+            sum_squares = psum_ss.tile([P, UNIT_HEADS, TOKEN_TILES, ONES_COLS], F32)
+            for h, n in enumerate(unit_heads(i)):
                 squares = squared[n]
                 for m in range(TOKEN_TILES):
                     nc.tensor.matmul(
-                        out=sum_squares[:, n, m, :], lhsT=squares[:, m * P : (m + 1) * P], rhs=ones[:],
+                        out=sum_squares[:, h, m, :], lhsT=squares[:, m * P : (m + 1) * P], rhs=ones[:],
                         start=True, stop=True,
                     )
+            sums_tiles[i] = sum_squares
 
         def norm_factors(i):
-            first = i * UNIT_HEADS
             rms = stats.tile([P, UNIT_HEADS, TOKEN_TILES], F32)
             nc.scalar.activation(
-                out=rms[:], in_=sum_squares[:, first : first + UNIT_HEADS, :, 0],
+                out=rms[:], in_=sums_tiles[i][:, :, :, 0],
                 func=ACT.Sqrt, bias=EPS, scale=1.0 / HEAD,
             )
             rstd = stats.tile([P, UNIT_HEADS, TOKEN_TILES], F32)

@@ -78,8 +78,6 @@ def tile_llamacausalselfattention_pa_kernel(
 
         x_blocks = x.flatten_outer_dims().rearrange("(m p) k -> p m k", p=P)
         x_raw = xpool.tile([P, PASSES, TOKEN_TILES, K_PASS], BF16)
-        for c in range(PASSES):
-            nc.sync.dma_start(out=x_raw[:, c, :, :], in_=x_blocks[:, :, c * K_PASS : (c + 1) * K_PASS])
 
         def weight_columns(g):
             if g < Q_CHUNKS:
@@ -98,7 +96,10 @@ def tile_llamacausalselfattention_pa_kernel(
             )
             raw_tiles[j] = raw
 
-        for j in range(RAW_BUFS):
+        for c in range(PASSES):
+            nc.sync.dma_start(out=x_raw[:, c, :, :], in_=x_blocks[:, :, c * K_PASS : (c + 1) * K_PASS])
+            load_weight_tile(c)
+        for j in range(PASSES, RAW_BUFS):
             load_weight_tile(j)
 
         ident = const.tile([P, P], F32)
@@ -151,22 +152,17 @@ def tile_llamacausalselfattention_pa_kernel(
                 out=x_codes[:, c, :].bitcast(FP8X4), scales=x_scales[:, c, :], in_=x_grouped[:, c, :]
             )
 
-        for c in range(PASSES):
+        def turn_x(c):
             x_words = x_raw[:, c, :, :].bitcast(F32).rearrange("p m (w u) -> p m u w", u=2)
-            for half, copy_out in enumerate((nc.vector.tensor_copy, nc.scalar.copy)):
+            for half in range(2):
                 turned = psum_acc.tile([P, 2, 2, P], F32, tag="acc")
                 for m2 in range(2):
                     for u in range(2):
                         nc.tensor.transpose(turned[:, m2, u, :], x_words[:, 2 * half + m2, u, :], ident[:])
-                copy_out(
+                nc.scalar.copy(
                     out=x_grouped_words[:, c, 2 * half : 2 * half + 2, :, :],
                     in_=turned[:].rearrange("p m u r -> p m r u"),
                 )
-            if c == 0:
-                build_tables()
-            else:
-                quantise_x(c - 1)
-        quantise_x(PASSES - 1)
 
         w_codes = [wmx.tile([P, PASSES, CHUNK], U32, align_bytes=64, name="w_codes%d" % g) for g in range(CHUNKS)]
         w_scales = [wmx.tile([P, PASSES, CHUNK], U8, align_bytes=64, name="w_scales%d" % g) for g in range(CHUNKS)]
@@ -197,7 +193,7 @@ def tile_llamacausalselfattention_pa_kernel(
                 regroup_weight_tile(j)
                 if j + RAW_BUFS < W_TILES:
                     load_weight_tile(j + RAW_BUFS)
-            if 1 <= j <= W_TILES:
+            if PASSES < j <= W_TILES:
                 quantise_weight_tile(j - 1)
 
         acc_tiles = {}
@@ -213,12 +209,13 @@ def tile_llamacausalselfattention_pa_kernel(
 
         def project(i):
             for n in unit_heads(i):
-                g, local = divmod(n, CHUNK_HEADS)
-                cols = slice(local * HEAD, (local + 1) * HEAD)
-                acc = psum_acc.tile([P, TOKENS], F32, tag="acc")
-                for c in range(PASSES):
+                acc_tiles[n] = psum_acc.tile([P, TOKENS], F32, tag="acc", name="acc")
+            for c in range(PASSES):
+                for n in unit_heads(i):
+                    g, local = divmod(n, CHUNK_HEADS)
+                    cols = slice(local * HEAD, (local + 1) * HEAD)
                     nc.tensor.matmul_mx(
-                        out=acc[:],
+                        out=acc_tiles[n][:],
                         lhsT=w_codes[g][:, c, cols].bitcast(FP8X4),
                         lhsT_scale=w_scales[g][:, c, cols],
                         rhs=x_codes[:, c, :].bitcast(FP8X4),
@@ -226,7 +223,6 @@ def tile_llamacausalselfattention_pa_kernel(
                         start=(c == 0),
                         stop=(c == PASSES - 1),
                     )
-                acc_tiles[n] = acc
 
         def rotate_terms(i):
             for n in unit_heads(i):
@@ -335,12 +331,18 @@ def tile_llamacausalselfattention_pa_kernel(
             )
 
         LEAD = PASSES + 3
-        for j in range(PASSES + 1):
-            prepare(j)
+        for c in range(PASSES):
+            turn_x(c)
+            if c == 0:
+                build_tables()
+            regroup_weight_tile(c)
+            load_weight_tile(c + RAW_BUFS)
+            quantise_x(c)
+            quantise_weight_tile(c)
         project(0)
-        square(0)
-        for j in range(PASSES + 1, LEAD):
+        for j in range(PASSES, LEAD):
             prepare(j)
+        square(0)
         for i in range(ROPE_UNITS):
             if i + 1 < ROPE_UNITS:
                 project(i + 1)

@@ -32,8 +32,13 @@ W_TILES = CHUNKS * PASSES
 ROPE_HEADS = Q_HEADS + KV_HEADS
 UNIT_HEADS = 2
 ROPE_UNITS = ROPE_HEADS // UNIT_HEADS
+UNIT_COLS = UNIT_HEADS * HEAD
+UNITS = CHUNKS * CHUNK // UNIT_COLS
 RAW_BUFS = 8
-VECTOR_COLS = 320
+UNIT_WORK = PASSES * UNIT_COLS
+GPSIMD_END = 384
+SCALAR_END = 704
+OPENING_SCALAR_COLS = 192
 ONES_COLS = 64
 GAIN_COL = ROPE_HEADS
 
@@ -48,11 +53,12 @@ def tile_llamacausalselfattention_pa_kernel(
         const = pools.enter_context(tc.tile_pool(name="const", bufs=1))
         xpool = pools.enter_context(tc.tile_pool(name="xpool", bufs=1))
         wraw = pools.enter_context(tc.tile_pool(name="wraw", bufs=RAW_BUFS))
-        wgrp = pools.enter_context(tc.tile_pool(name="wgrp", bufs=4))
+        wgrp = pools.enter_context(tc.tile_pool(name="wgrp", bufs=1))
         wmx = pools.enter_context(tc.tile_pool(name="wmx", bufs=1))
         work = pools.enter_context(tc.tile_pool(name="work", bufs=4))
         stats = pools.enter_context(tc.tile_pool(name="stats", bufs=4))
         outs = pools.enter_context(tc.tile_pool(name="outs", bufs=3))
+        vout = pools.enter_context(tc.tile_pool(name="vout", bufs=4))
         psum_acc = pools.enter_context(tc.psum_pool(name="psum_acc", bufs=4))
         psum_back = pools.enter_context(tc.psum_pool(name="psum_back", bufs=3))
         psum_ss = pools.enter_context(tc.psum_pool(name="psum_ss", bufs=1))
@@ -74,7 +80,9 @@ def tile_llamacausalselfattention_pa_kernel(
         nc.scalar.dma_start(out=cos_sin[:, 0, :, :], in_=freqs_cos.rearrange("(a p) j -> p a j", p=P))
         nc.scalar.dma_start(out=cos_sin[:, 1, :, :], in_=freqs_sin.rearrange("(a p) j -> p a j", p=P))
         bv_all = const.tile([P, CHUNK], BF16)
-        nc.scalar.dma_start(out=bv_all[:], in_=bv.partition_broadcast(P))
+        warm = const.tile([P, 2], F32)
+        nc.vector.memset(warm[:], 1.0)
+        nc.scalar.activation(out=warm[:, 1:2], in_=warm[:, 0:1], func=ACT.Abs_reciprocal_sqrt)
 
         x_blocks = x.flatten_outer_dims().rearrange("(m p) k -> p m k", p=P)
         x_raw = xpool.tile([P, PASSES, TOKEN_TILES, K_PASS], BF16)
@@ -96,8 +104,13 @@ def tile_llamacausalselfattention_pa_kernel(
             )
             raw_tiles[j] = raw
 
-        for c in range(PASSES):
+        def load_x(c):
             nc.sync.dma_start(out=x_raw[:, c, :, :], in_=x_blocks[:, :, c * K_PASS : (c + 1) * K_PASS])
+
+        load_x(0)
+        for c in range(PASSES):
+            if c + 1 < PASSES:
+                load_x(c + 1)
             load_weight_tile(c)
         for j in range(PASSES, RAW_BUFS):
             load_weight_tile(j)
@@ -129,17 +142,16 @@ def tile_llamacausalselfattention_pa_kernel(
         def build_tables():
             rows_ps = psum_back.tile([P, P], F32, tag="back")
             nc.tensor.transpose(rows_ps[:], rows_f32[:], ident[:])
-            nc.scalar.copy(out=per_feature[:], in_=rows_ps[:])
+            nc.vector.tensor_copy(out=per_feature[:], in_=rows_ps[:])
             spread_ps = psum_back.tile([P, 2, SEQ_TILES, P], F32, tag="back")
             for s in range(2):
                 for a in range(SEQ_TILES):
                     nc.tensor.transpose(spread_ps[:, s, a, :], spread[:, s, a, :], ident[:])
             for w in range(2):
-                nc.scalar.activation(
+                nc.vector.tensor_scalar_mul(
                     out=tables[:, w, :, :],
-                    in_=spread_ps[:].rearrange("p s a t -> p s (a t)"),
-                    func=ACT.Copy,
-                    scale=per_feature[:, GAIN_COL + w : GAIN_COL + w + 1],
+                    in0=spread_ps[:].rearrange("p s a t -> p s (a t)"),
+                    scalar1=per_feature[:, GAIN_COL + w : GAIN_COL + w + 1],
                 )
 
         x_grouped = xpool.tile([P, PASSES, TOKENS * PACK], BF16, align_bytes=64)
@@ -155,7 +167,7 @@ def tile_llamacausalselfattention_pa_kernel(
         def turn_x(c):
             x_words = x_raw[:, c, :, :].bitcast(F32).rearrange("p m (w u) -> p m u w", u=2)
             for half in range(2):
-                turned = psum_acc.tile([P, 2, 2, P], F32, tag="acc")
+                turned = psum_back.tile([P, 2, 2, P], F32, tag="back")
                 for m2 in range(2):
                     for u in range(2):
                         nc.tensor.transpose(turned[:, m2, u, :], x_words[:, 2 * half + m2, u, :], ident[:])
@@ -164,37 +176,46 @@ def tile_llamacausalselfattention_pa_kernel(
                     in_=turned[:].rearrange("p m u r -> p m r u"),
                 )
 
-        w_codes = [wmx.tile([P, PASSES, CHUNK], U32, align_bytes=64, name="w_codes%d" % g) for g in range(CHUNKS)]
-        w_scales = [wmx.tile([P, PASSES, CHUNK], U8, align_bytes=64, name="w_scales%d" % g) for g in range(CHUNKS)]
+        w_codes = [wmx.tile([P, PASSES, UNIT_COLS], U32, align_bytes=64, name="w_codes%d" % u) for u in range(UNITS)]
+        w_scales = [wmx.tile([P, PASSES, UNIT_COLS], U8, align_bytes=64, name="w_scales%d" % u) for u in range(UNITS)]
 
-        def regroup_weight_tile(j):
-            raw = raw_tiles[j]
-            grouped = wgrp.tile([P, CHUNK, PACK], BF16, align_bytes=64)
-            nc.vector.tensor_copy(
-                out=grouped[:, :VECTOR_COLS, :].rearrange("p (n i) t -> p n t i", i=4),
-                in_=raw[:, :, :VECTOR_COLS].rearrange("p t (n i) -> p n t i", i=4),
-            )
-            nc.scalar.copy(
-                out=grouped[:, VECTOR_COLS:, :].rearrange("p (n i) t -> p n t i", i=4),
-                in_=raw[:, :, VECTOR_COLS:].rearrange("p t (n i) -> p n t i", i=4),
-            )
-            grouped_tiles[j] = grouped
+        def grouped_of(u):
+            if u not in grouped_tiles:
+                grouped_tiles[u] = wgrp.tile(
+                    [P, PASSES, UNIT_COLS, PACK], BF16, align_bytes=64, name="grouped_first" if u == 0 else "grouped"
+                )
+            return grouped_tiles[u]
 
-        def quantise_weight_tile(j):
-            g, c = divmod(j, PASSES)
+        def regroup(u, engine, lo, hi):
+            g, half = divmod(u, CHUNK // UNIT_COLS)
+            for c in range(PASSES):
+                a = max(lo, c * UNIT_COLS) - c * UNIT_COLS
+                b = min(hi, (c + 1) * UNIT_COLS) - c * UNIT_COLS
+                if a >= b:
+                    continue
+                dst = grouped_of(u)[:, c, a:b, :].rearrange("p (n i) t -> p n t i", i=4)
+                src = raw_tiles[g * PASSES + c][:, :, half * UNIT_COLS + a : half * UNIT_COLS + b].rearrange(
+                    "p t (n i) -> p n t i", i=4
+                )
+                if engine == "vector":
+                    nc.vector.tensor_copy(out=dst, in_=src)
+                elif engine == "scalar":
+                    nc.scalar.copy(out=dst, in_=src)
+                else:
+                    nc.gpsimd.tensor_scalar(out=dst, in0=src, scalar1=1.0, scalar2=0.0, op0=ALU.mult, op1=ALU.add)
+
+        def load_behind(u):
+            g, half = divmod(u, CHUNK // UNIT_COLS)
+            if half == 1 and g + 2 < CHUNKS:
+                for c in range(PASSES):
+                    load_weight_tile((g + 2) * PASSES + c)
+
+        def quantise_unit(u, first_pass=0, last_pass=PASSES):
             nc.vector.quantize_mx(
-                out=w_codes[g][:, c, :].bitcast(FP8X4),
-                scales=w_scales[g][:, c, :],
-                in_=grouped_tiles[j][:].rearrange("p n t -> p (n t)"),
+                out=w_codes[u][:, first_pass:last_pass, :].rearrange("p c n -> p (c n)").bitcast(FP8X4),
+                scales=w_scales[u][:, first_pass:last_pass, :].rearrange("p c n -> p (c n)"),
+                in_=grouped_of(u)[:, first_pass:last_pass, :, :].rearrange("p c n t -> p (c n t)"),
             )
-
-        def prepare(j):
-            if j < W_TILES:
-                regroup_weight_tile(j)
-                if j + RAW_BUFS < W_TILES:
-                    load_weight_tile(j + RAW_BUFS)
-            if PASSES < j <= W_TILES:
-                quantise_weight_tile(j - 1)
 
         acc_tiles = {}
         rotated = {}
@@ -207,84 +228,98 @@ def tile_llamacausalselfattention_pa_kernel(
         def unit_heads(i):
             return range(i * UNIT_HEADS, (i + 1) * UNIT_HEADS)
 
-        def project(i):
-            for n in unit_heads(i):
-                acc_tiles[n] = psum_acc.tile([P, TOKENS], F32, tag="acc", name="acc")
+        def one_pass(n, c):
+            u, h = divmod(n, UNIT_HEADS)
+            cols = slice(h * HEAD, (h + 1) * HEAD)
+            nc.tensor.matmul_mx(
+                out=acc_tiles[n][:],
+                lhsT=w_codes[u][:, c, cols].bitcast(FP8X4),
+                lhsT_scale=w_scales[u][:, c, cols],
+                rhs=x_codes[:, c, :].bitcast(FP8X4),
+                rhs_scale=x_scales[:, c, :],
+                start=(c == 0),
+                stop=(c == PASSES - 1),
+            )
+
+        def project_head(n):
+            acc_tiles[n] = psum_acc.tile([P, TOKENS], F32, tag="acc", name="acc")
             for c in range(PASSES):
-                for n in unit_heads(i):
-                    g, local = divmod(n, CHUNK_HEADS)
-                    cols = slice(local * HEAD, (local + 1) * HEAD)
+                one_pass(n, c)
+
+        def project_v(n):
+            u, h = divmod(n, UNIT_HEADS)
+            acc_tiles[n] = psum_acc.tile([P, 2, UNIT_COLS], F32, tag="acc", name="acc")
+            for mm in range(2):
+                tokens = slice((2 * h + mm) * P, (2 * h + mm + 1) * P)
+                for c in range(PASSES):
                     nc.tensor.matmul_mx(
-                        out=acc_tiles[n][:],
-                        lhsT=w_codes[g][:, c, cols].bitcast(FP8X4),
-                        lhsT_scale=w_scales[g][:, c, cols],
-                        rhs=x_codes[:, c, :].bitcast(FP8X4),
-                        rhs_scale=x_scales[:, c, :],
+                        out=acc_tiles[n][:, mm, :],
+                        lhsT=x_codes[:, c, tokens].bitcast(FP8X4),
+                        lhsT_scale=x_scales[:, c, tokens],
+                        rhs=w_codes[u][:, c, :].bitcast(FP8X4),
+                        rhs_scale=w_scales[u][:, c, :],
                         start=(c == 0),
                         stop=(c == PASSES - 1),
                     )
 
-        def rotate_terms(i):
-            for n in unit_heads(i):
-                acc = acc_tiles[n]
-                bias = per_feature[:, n : n + 1]
-                w = 0 if n < Q_HEADS else 1
-                by_cos = work.tile([P, TOKENS], F32)
-                by_sin = work.tile([P, TOKENS], F32)
-                for s, term in enumerate((by_cos, by_sin)):
-                    nc.vector.scalar_tensor_tensor(
-                        out=term[:].rearrange("p (b t) -> p b t", b=BATCH),
-                        in0=acc[:].rearrange("p (b t) -> p b t", b=BATCH),
-                        scalar=bias,
-                        in1=tables[:, w, s, :].unsqueeze(1).to_broadcast([P, BATCH, SEQ]),
-                        op0=ALU.add,
-                        op1=ALU.mult,
-                    )
-                rotated[n] = (by_cos, by_sin)
+        def start_head(n):
+            if n < ROPE_HEADS:
+                project_head(n)
+            else:
+                project_v(n)
 
-        def square(i):
-            for n in unit_heads(i):
-                squares = work.tile([P, TOKENS], F32)
-                nc.scalar.activation(
-                    out=squares[:], in_=acc_tiles[n][:], func=ACT.Square, bias=per_feature[:, n : n + 1], scale=1.0
+        def rotate_head(n):
+            acc = acc_tiles[n]
+            bias = per_feature[:, n : n + 1]
+            w = 0 if n < Q_HEADS else 1
+            by_cos = work.tile([P, TOKENS], F32)
+            by_sin = work.tile([P, TOKENS], F32)
+            for s, term in enumerate((by_cos, by_sin)):
+                nc.vector.scalar_tensor_tensor(
+                    out=term[:].rearrange("p (b t) -> p b t", b=BATCH),
+                    in0=acc[:].rearrange("p (b t) -> p b t", b=BATCH),
+                    scalar=bias,
+                    in1=tables[:, w, s, :].unsqueeze(1).to_broadcast([P, BATCH, SEQ]),
+                    op0=ALU.add,
+                    op1=ALU.mult,
                 )
-                squared[n] = squares
+            rotated[n] = (by_cos, by_sin)
 
-        def turn_back(i):
-            for n in unit_heads(i):
-                by_cos, by_sin = rotated[n]
-                back = psum_back.tile([P, TOKEN_TILES, HEAD], F32, tag="back")
-                for m in range(TOKEN_TILES):
-                    tokens = slice(m * P, (m + 1) * P)
-                    nc.tensor.matmul(
-                        out=back[:, m, :], lhsT=by_cos[:, tokens], rhs=ident[:],
-                        is_transpose=True, start=True, stop=False,
-                    )
-                    nc.tensor.matmul(
-                        out=back[:, m, :], lhsT=by_sin[:, tokens], rhs=swap[:],
-                        is_transpose=True, start=False, stop=True,
-                    )
-                back_tiles[n] = back
+        def square_head(n):
+            squares = work.tile([P, TOKENS], F32)
+            nc.scalar.activation(
+                out=squares[:], in_=acc_tiles[n][:], func=ACT.Square, bias=per_feature[:, n : n + 1], scale=1.0
+            )
+            squared[n] = squares
 
-        def sum_over_features(i):
-            sum_squares = psum_ss.tile([P, UNIT_HEADS, TOKEN_TILES, ONES_COLS], F32)
-            for h, n in enumerate(unit_heads(i)):
-                squares = squared[n]
-                for m in range(TOKEN_TILES):
-                    nc.tensor.matmul(
-                        out=sum_squares[:, h, m, :], lhsT=squares[:, m * P : (m + 1) * P], rhs=ones[:],
-                        start=True, stop=True,
-                    )
-            sums_tiles[i] = sum_squares
+        def turn_back_head(n):
+            i, h = divmod(n, UNIT_HEADS)
+            if i not in sums_tiles:
+                sums_tiles[i] = psum_ss.tile([P, UNIT_HEADS, TOKEN_TILES, ONES_COLS], F32, name="sum_squares")
+            by_cos, by_sin = rotated[n]
+            back = psum_back.tile([P, TOKEN_TILES, HEAD], F32, tag="back")
+            for m in range(TOKEN_TILES):
+                tokens = slice(m * P, (m + 1) * P)
+                nc.tensor.matmul(
+                    out=back[:, m, :], lhsT=by_cos[:, tokens], rhs=ident[:],
+                    is_transpose=True, start=True, stop=False,
+                )
+                nc.tensor.matmul(
+                    out=back[:, m, :], lhsT=by_sin[:, tokens], rhs=swap[:],
+                    is_transpose=True, start=False, stop=True,
+                )
+                nc.tensor.matmul(
+                    out=sums_tiles[i][:, h, m, :], lhsT=squared[n][:, tokens], rhs=ones[:],
+                    start=True, stop=True,
+                )
+            back_tiles[n] = back
 
         def norm_factors(i):
-            rms = stats.tile([P, UNIT_HEADS, TOKEN_TILES], F32)
-            nc.scalar.activation(
-                out=rms[:], in_=sums_tiles[i][:, :, :, 0],
-                func=ACT.Sqrt, bias=EPS, scale=1.0 / HEAD,
-            )
             rstd = stats.tile([P, UNIT_HEADS, TOKEN_TILES], F32)
-            nc.vector.reciprocal(out=rstd[:], in_=rms[:])
+            nc.scalar.activation(
+                out=rstd[:], in_=sums_tiles[i][:, :, :, 0],
+                func=ACT.Abs_reciprocal_sqrt, bias=EPS, scale=1.0 / HEAD,
+            )
             rstd_tiles[i] = rstd
 
         def finish(i):
@@ -308,57 +343,69 @@ def tile_llamacausalselfattention_pa_kernel(
                     dest = out_1.rearrange("b t h d -> (b t) (h d)")
                 nc.scalar.dma_start(out=dest.rearrange("(m p) n -> p m n", p=P), in_=result[:])
 
-        def project_v(m):
-            acc = psum_acc.tile([P, CHUNK], F32, tag="acc")
-            tokens = slice(m * P, (m + 1) * P)
-            for c in range(PASSES):
-                nc.tensor.matmul_mx(
-                    out=acc[:],
-                    lhsT=x_codes[:, c, tokens].bitcast(FP8X4),
-                    lhsT_scale=x_scales[:, c, tokens],
-                    rhs=w_codes[V_CHUNK][:, c, :].bitcast(FP8X4),
-                    rhs_scale=w_scales[V_CHUNK][:, c, :],
-                    start=(c == 0),
-                    stop=(c == PASSES - 1),
-                )
-            return acc
-
-        def finish_v(m, acc):
-            v_rows = outs.tile([P, CHUNK], F32)
-            nc.vector.tensor_tensor(out=v_rows[:], in0=acc[:], in1=bv_all[:], op=ALU.add)
+        def finish_v(n):
+            u, h = divmod(n, UNIT_HEADS)
+            cols = slice((u - ROPE_UNITS) * UNIT_COLS, (u - ROPE_UNITS + 1) * UNIT_COLS)
+            v_rows = vout.tile([P, 2, UNIT_COLS], F32)
+            nc.vector.tensor_tensor(
+                out=v_rows[:], in0=acc_tiles[n][:],
+                in1=bv_all[:, cols].unsqueeze(1).to_broadcast([P, 2, UNIT_COLS]), op=ALU.add,
+            )
             nc.sync.dma_start(
-                out=out_2.rearrange("b t h d -> (b t) (h d)")[m * P : (m + 1) * P, :], in_=v_rows[:]
+                out=out_2.rearrange("b t h d -> (b t) (h d)")[2 * h * P : (2 * h + 2) * P, cols].rearrange(
+                    "(m p) n -> p m n", p=P
+                ),
+                in_=v_rows[:],
             )
 
-        LEAD = PASSES + 3
+        build_tables()
+        for n in unit_heads(0):
+            acc_tiles[n] = psum_acc.tile([P, TOKENS], F32, tag="acc", name="acc")
         for c in range(PASSES):
             turn_x(c)
-            if c == 0:
-                build_tables()
-            regroup_weight_tile(c)
-            load_weight_tile(c + RAW_BUFS)
+            if c >= 1:
+                for n in unit_heads(0):
+                    one_pass(n, c - 1)
+            regroup(0, "vector", c * UNIT_COLS, (c + 1) * UNIT_COLS)
+            regroup(1, "scalar", c * UNIT_COLS, c * UNIT_COLS + OPENING_SCALAR_COLS)
             quantise_x(c)
-            quantise_weight_tile(c)
-        project(0)
-        for j in range(PASSES, LEAD):
-            prepare(j)
-        square(0)
+            quantise_unit(0, c, c + 1)
+            regroup(1, "vector", c * UNIT_COLS + OPENING_SCALAR_COLS, (c + 1) * UNIT_COLS)
+        for n in unit_heads(0):
+            one_pass(n, PASSES - 1)
+        load_behind(1)
+        quantise_unit(1)
+        for n in unit_heads(0):
+            square_head(n)
         for i in range(ROPE_UNITS):
-            if i + 1 < ROPE_UNITS:
-                project(i + 1)
-            else:
-                v_acc = [project_v(m) for m in range(UNIT_HEADS)]
+            first, second = unit_heads(i)
+            prep = i + 2
+            if prep < UNITS:
+                regroup(prep, "gpsimd", 0, GPSIMD_END)
+                regroup(prep, "scalar", GPSIMD_END, SCALAR_END)
+            start_head(first + UNIT_HEADS)
             if i >= 1:
+                norm_factors(i - 1)
                 finish(i - 1)
-            rotate_terms(i)
-            sum_over_features(i)
-            turn_back(i)
-            prepare(LEAD + 2 * i)
-            prepare(LEAD + 2 * i + 1)
-            norm_factors(i)
+            if i == 2:
+                nc.scalar.dma_start(out=bv_all[:], in_=bv.partition_broadcast(P))
+            rotate_head(first)
+            rotate_head(second)
+            turn_back_head(first)
+            start_head(second + UNIT_HEADS)
             if i + 1 < ROPE_UNITS:
-                square(i + 1)
-        v_acc.extend([project_v(m) for m in range(UNIT_HEADS, TOKEN_TILES)])
+                square_head(first + UNIT_HEADS)
+            turn_back_head(second)
+            if i + 1 < ROPE_UNITS:
+                square_head(second + UNIT_HEADS)
+            if prep < UNITS:
+                regroup(prep, "vector", SCALAR_END, UNIT_WORK)
+                load_behind(prep)
+                quantise_unit(prep)
+        for n in unit_heads(UNITS - 1):
+            start_head(n)
+        norm_factors(ROPE_UNITS - 1)
         finish(ROPE_UNITS - 1)
-        for m in range(TOKEN_TILES):
-            finish_v(m, v_acc[m])
+        for u in range(ROPE_UNITS, UNITS):
+            for n in unit_heads(u):
+                finish_v(n)

@@ -39,7 +39,7 @@ UNIT_WORK = PASSES * UNIT_COLS
 GPSIMD_END = 384
 SCALAR_END = 704
 OPENING_SCALAR_COLS = 192
-ONES_COLS = 64
+ONES_COLS = 16
 GAIN_COL = ROPE_HEADS
 
 FLOPS = 2 * TOKENS * WIDTH * (Q_HEADS + 2 * KV_HEADS) * HEAD

@@ -64,26 +64,6 @@ def tile_llamacausalselfattention_pa_kernel(
         psum_ss = pools.enter_context(tc.psum_pool(name="psum_ss", bufs=1))
         pools.enter_context(tc.manual_schedule())
 
-        rows_bf = const.tile([P, P], BF16)
-        nc.vector.memset(rows_bf[:], 0.0)
-        nc.scalar.dma_start(out=rows_bf[0:Q_HEADS, :], in_=bq.rearrange("(h d) -> h d", d=HEAD))
-        nc.scalar.dma_start(
-            out=rows_bf[Q_HEADS:ROPE_HEADS, :], in_=bk.rearrange("(h d) -> h d", d=HEAD)
-        )
-        nc.scalar.dma_start(
-            out=rows_bf[GAIN_COL : GAIN_COL + 1, :], in_=qn_w.rearrange("(o d) -> o d", o=1)
-        )
-        nc.scalar.dma_start(
-            out=rows_bf[GAIN_COL + 1 : GAIN_COL + 2, :], in_=kn_w.rearrange("(o d) -> o d", o=1)
-        )
-        cos_sin = const.tile([P, 2, SEQ_TILES, HEAD // 2], BF16)
-        nc.scalar.dma_start(out=cos_sin[:, 0, :, :], in_=freqs_cos.rearrange("(a p) j -> p a j", p=P))
-        nc.scalar.dma_start(out=cos_sin[:, 1, :, :], in_=freqs_sin.rearrange("(a p) j -> p a j", p=P))
-        bv_all = const.tile([P, CHUNK], BF16)
-        warm = const.tile([P, 2], F32)
-        nc.vector.memset(warm[:], 1.0)
-        nc.scalar.activation(out=warm[:, 1:2], in_=warm[:, 0:1], func=ACT.Abs_reciprocal_sqrt)
-
         x_blocks = x.flatten_outer_dims().rearrange("(m p) k -> p m k", p=P)
         x_raw = xpool.tile([P, PASSES, TOKEN_TILES, K_PASS], BF16)
 
@@ -107,16 +87,36 @@ def tile_llamacausalselfattention_pa_kernel(
         def load_x(c):
             nc.sync.dma_start(out=x_raw[:, c, :, :], in_=x_blocks[:, :, c * K_PASS : (c + 1) * K_PASS])
 
+        rows_bf = const.tile([P, P], BF16)
+        nc.vector.memset(rows_bf[:], 0.0)
+        cos_sin = const.tile([P, 2, SEQ_TILES, HEAD // 2], BF16)
+        bv_all = const.tile([P, CHUNK], BF16)
         load_x(0)
-        for c in range(PASSES):
-            if c + 1 < PASSES:
-                load_x(c + 1)
-            load_weight_tile(c)
-        for j in range(PASSES, RAW_BUFS):
+        load_x(1)
+        load_weight_tile(0)
+        load_x(2)
+        load_weight_tile(1)
+        nc.scalar.dma_start(out=rows_bf[0:Q_HEADS, :], in_=bq.rearrange("(h d) -> h d", d=HEAD))
+        nc.scalar.dma_start(
+            out=rows_bf[Q_HEADS:ROPE_HEADS, :], in_=bk.rearrange("(h d) -> h d", d=HEAD)
+        )
+        nc.scalar.dma_start(
+            out=rows_bf[GAIN_COL : GAIN_COL + 1, :], in_=qn_w.rearrange("(o d) -> o d", o=1)
+        )
+        load_x(3)
+        for j in range(2, RAW_BUFS):
             load_weight_tile(j)
+        warm = const.tile([P, 2], F32)
+        nc.vector.memset(warm[:], 1.0)
+        nc.scalar.activation(out=warm[:, 1:2], in_=warm[:, 0:1], func=ACT.Abs_reciprocal_sqrt)
 
         ident = const.tile([P, P], F32)
         make_identity(nc, ident[:])
+        nc.gpsimd.dma_start(
+            out=rows_bf[GAIN_COL + 1 : GAIN_COL + 2, :], in_=kn_w.rearrange("(o d) -> o d", o=1)
+        )
+        nc.gpsimd.dma_start(out=cos_sin[:, 0, :, :], in_=freqs_cos.rearrange("(a p) j -> p a j", p=P))
+        nc.gpsimd.dma_start(out=cos_sin[:, 1, :, :], in_=freqs_sin.rearrange("(a p) j -> p a j", p=P))
         swap = const.tile([P, P], F32)
         ident_pairs = ident[:].rearrange("p (j two) -> p j two", two=2)
         swap_pairs = swap[:].rearrange("p (j two) -> p j two", two=2)
@@ -126,31 +126,38 @@ def tile_llamacausalselfattention_pa_kernel(
         nc.vector.memset(ones[:], 1.0)
 
         rows_f32 = const.tile([P, P], F32)
-        nc.vector.tensor_copy(out=rows_f32[:], in_=rows_bf[:])
         spread = const.tile([P, 2, SEQ_TILES, HEAD], F32)
-        cos_pairs = spread[:, 0, :, :].rearrange("p a (j two) -> p a j two", two=2)
-        sin_pairs = spread[:, 1, :, :].rearrange("p a (j two) -> p a j two", two=2)
-        nc.vector.tensor_copy(
-            out=cos_pairs,
-            in_=cos_sin[:, 0, :, :].unsqueeze(3).to_broadcast([P, SEQ_TILES, HEAD // 2, 2]),
-        )
-        nc.vector.tensor_copy(out=sin_pairs[:, :, :, 0], in_=cos_sin[:, 1, :, :])
-        nc.vector.tensor_scalar_mul(out=sin_pairs[:, :, :, 1], in0=cos_sin[:, 1, :, :], scalar1=-1.0)
         per_feature = const.tile([P, P], F32)
         tables = const.tile([P, 2, 2, SEQ], F32)
+        table_banks = {}
 
-        def build_tables():
+        def spread_small_vectors():
+            nc.vector.tensor_copy(out=rows_f32[:], in_=rows_bf[:])
+            cos_pairs = spread[:, 0, :, :].rearrange("p a (j two) -> p a j two", two=2)
+            sin_pairs = spread[:, 1, :, :].rearrange("p a (j two) -> p a j two", two=2)
+            nc.vector.tensor_copy(
+                out=cos_pairs,
+                in_=cos_sin[:, 0, :, :].unsqueeze(3).to_broadcast([P, SEQ_TILES, HEAD // 2, 2]),
+            )
+            nc.vector.tensor_copy(out=sin_pairs[:, :, :, 0], in_=cos_sin[:, 1, :, :])
+            nc.vector.tensor_scalar_mul(out=sin_pairs[:, :, :, 1], in0=cos_sin[:, 1, :, :], scalar1=-1.0)
+
+        def turn_tables():
             rows_ps = psum_back.tile([P, P], F32, tag="back")
             nc.tensor.transpose(rows_ps[:], rows_f32[:], ident[:])
-            nc.vector.tensor_copy(out=per_feature[:], in_=rows_ps[:])
             spread_ps = psum_back.tile([P, 2, SEQ_TILES, P], F32, tag="back")
             for s in range(2):
                 for a in range(SEQ_TILES):
                     nc.tensor.transpose(spread_ps[:, s, a, :], spread[:, s, a, :], ident[:])
+            table_banks["rows"] = rows_ps
+            table_banks["spread"] = spread_ps
+
+        def scale_tables():
+            nc.vector.tensor_copy(out=per_feature[:], in_=table_banks["rows"][:])
             for w in range(2):
                 nc.vector.tensor_scalar_mul(
                     out=tables[:, w, :, :],
-                    in0=spread_ps[:].rearrange("p s a t -> p s (a t)"),
+                    in0=table_banks["spread"][:].rearrange("p s a t -> p s (a t)"),
                     scalar1=per_feature[:, GAIN_COL + w : GAIN_COL + w + 1],
                 )
 
@@ -358,10 +365,14 @@ def tile_llamacausalselfattention_pa_kernel(
                 in_=v_rows[:],
             )
 
-        build_tables()
         for n in unit_heads(0):
             acc_tiles[n] = psum_acc.tile([P, TOKENS], F32, tag="acc", name="acc")
         for c in range(PASSES):
+            if c == 2:
+                spread_small_vectors()
+            if c == 3:
+                turn_tables()
+                scale_tables()
             turn_x(c)
             if c >= 1:
                 for n in unit_heads(0):

@@ -39,7 +39,7 @@ UNIT_WORK = PASSES * UNIT_COLS
 GPSIMD_END = 384
 SCALAR_END = 704
 OPENING_SCALAR_COLS = 192
-ONES_COLS = 16
+ONES_COLS = 64
 GAIN_COL = ROPE_HEADS
 
 FLOPS = 2 * TOKENS * WIDTH * (Q_HEADS + 2 * KV_HEADS) * HEAD
@@ -132,20 +132,20 @@ def tile_llamacausalselfattention_pa_kernel(
         table_banks = {}
 
         def spread_small_vectors():
-            nc.vector.tensor_copy(out=rows_f32[:], in_=rows_bf[:])
             cos_pairs = spread[:, 0, :, :].rearrange("p a (j two) -> p a j two", two=2)
             sin_pairs = spread[:, 1, :, :].rearrange("p a (j two) -> p a j two", two=2)
-            nc.vector.tensor_copy(
-                out=cos_pairs,
-                in_=cos_sin[:, 0, :, :].unsqueeze(3).to_broadcast([P, SEQ_TILES, HEAD // 2, 2]),
-            )
-            nc.vector.tensor_copy(out=sin_pairs[:, :, :, 0], in_=cos_sin[:, 1, :, :])
-            nc.vector.tensor_scalar_mul(out=sin_pairs[:, :, :, 1], in0=cos_sin[:, 1, :, :], scalar1=-1.0)
+            for out, in0, factor in (
+                (rows_f32[:], rows_bf[:], 1.0),
+                (cos_pairs, cos_sin[:, 0, :, :].unsqueeze(3).to_broadcast([P, SEQ_TILES, HEAD // 2, 2]), 1.0),
+                (sin_pairs[:, :, :, 0], cos_sin[:, 1, :, :], 1.0),
+                (sin_pairs[:, :, :, 1], cos_sin[:, 1, :, :], -1.0),
+            ):
+                nc.gpsimd.tensor_scalar(out=out, in0=in0, scalar1=factor, scalar2=0.0, op0=ALU.mult, op1=ALU.add)
 
         def turn_tables():
-            rows_ps = psum_back.tile([P, P], F32, tag="back")
+            rows_ps = psum_acc.tile([P, P], F32, tag="acc")
             nc.tensor.transpose(rows_ps[:], rows_f32[:], ident[:])
-            spread_ps = psum_back.tile([P, 2, SEQ_TILES, P], F32, tag="back")
+            spread_ps = psum_acc.tile([P, 2, SEQ_TILES, P], F32, tag="acc")
             for s in range(2):
                 for a in range(SEQ_TILES):
                     nc.tensor.transpose(spread_ps[:, s, a, :], spread[:, s, a, :], ident[:])
@@ -153,12 +153,13 @@ def tile_llamacausalselfattention_pa_kernel(
             table_banks["spread"] = spread_ps
 
         def scale_tables():
-            nc.vector.tensor_copy(out=per_feature[:], in_=table_banks["rows"][:])
+            nc.scalar.copy(out=per_feature[:], in_=table_banks["rows"][:])
             for w in range(2):
-                nc.vector.tensor_scalar_mul(
+                nc.scalar.activation(
                     out=tables[:, w, :, :],
-                    in0=table_banks["spread"][:].rearrange("p s a t -> p s (a t)"),
-                    scalar1=per_feature[:, GAIN_COL + w : GAIN_COL + w + 1],
+                    in_=table_banks["spread"][:].rearrange("p s a t -> p s (a t)"),
+                    func=ACT.Copy,
+                    scale=per_feature[:, GAIN_COL + w : GAIN_COL + w + 1],
                 )
 
         x_grouped = xpool.tile([P, PASSES, TOKENS * PACK], BF16, align_bytes=64)
@@ -365,14 +366,10 @@ def tile_llamacausalselfattention_pa_kernel(
                 in_=v_rows[:],
             )
 
+        spread_small_vectors()
         for n in unit_heads(0):
             acc_tiles[n] = psum_acc.tile([P, TOKENS], F32, tag="acc", name="acc")
         for c in range(PASSES):
-            if c == 2:
-                spread_small_vectors()
-            if c == 3:
-                turn_tables()
-                scale_tables()
             turn_x(c)
             if c >= 1:
                 for n in unit_heads(0):
@@ -381,10 +378,13 @@ def tile_llamacausalselfattention_pa_kernel(
             regroup(1, "scalar", c * UNIT_COLS, c * UNIT_COLS + OPENING_SCALAR_COLS)
             quantise_x(c)
             quantise_unit(0, c, c + 1)
-            regroup(1, "vector", c * UNIT_COLS + OPENING_SCALAR_COLS, (c + 1) * UNIT_COLS)
+        turn_tables()
         for n in unit_heads(0):
             one_pass(n, PASSES - 1)
+        for c in range(PASSES):
+            regroup(1, "vector", c * UNIT_COLS + OPENING_SCALAR_COLS, (c + 1) * UNIT_COLS)
         load_behind(1)
+        scale_tables()
         quantise_unit(1)
         for n in unit_heads(0):
             square_head(n)
@@ -400,10 +400,10 @@ def tile_llamacausalselfattention_pa_kernel(
                 finish(i - 1)
             if i == 2:
                 nc.scalar.dma_start(out=bv_all[:], in_=bv.partition_broadcast(P))
+            start_head(second + UNIT_HEADS)
             rotate_head(first)
             rotate_head(second)
             turn_back_head(first)
-            start_head(second + UNIT_HEADS)
             if i + 1 < ROPE_UNITS:
                 square_head(first + UNIT_HEADS)
             turn_back_head(second)

@@ -306,8 +306,17 @@ def tile_llamacausalselfattention_pa_kernel(
                 sums_tiles[i] = psum_ss.tile([P, UNIT_HEADS, TOKEN_TILES, ONES_COLS], F32, name="sum_squares")
             by_cos, by_sin = rotated[n]
             back = psum_back.tile([P, TOKEN_TILES, HEAD], F32, tag="back")
+
+            def sum_tile(m):
+                nc.tensor.matmul(
+                    out=sums_tiles[i][:, h, m, :], lhsT=squared[n][:, m * P : (m + 1) * P], rhs=ones[:],
+                    start=True, stop=True,
+                )
+
             for m in range(TOKEN_TILES):
                 tokens = slice(m * P, (m + 1) * P)
+                if h == 0:
+                    sum_tile(m)
                 nc.tensor.matmul(
                     out=back[:, m, :], lhsT=by_cos[:, tokens], rhs=ident[:],
                     is_transpose=True, start=True, stop=False,
@@ -316,10 +325,8 @@ def tile_llamacausalselfattention_pa_kernel(
                     out=back[:, m, :], lhsT=by_sin[:, tokens], rhs=swap[:],
                     is_transpose=True, start=False, stop=True,
                 )
-                nc.tensor.matmul(
-                    out=sums_tiles[i][:, h, m, :], lhsT=squared[n][:, tokens], rhs=ones[:],
-                    start=True, stop=True,
-                )
+                if h == 1:
+                    sum_tile(m)
             back_tiles[n] = back
 
         def norm_factors(i):
@@ -344,11 +351,14 @@ def tile_llamacausalselfattention_pa_kernel(
                         func=ACT.Copy,
                         scale=rstd_tiles[i][:, h, m : m + 1],
                     )
-            if (i + 1) * UNIT_HEADS % CHUNK_HEADS == 0:
-                if g < Q_CHUNKS:
-                    dest = out_0.rearrange("b t h d -> (b t) (h d)")[:, g * CHUNK : (g + 1) * CHUNK]
-                else:
-                    dest = out_1.rearrange("b t h d -> (b t) (h d)")
+            if g == K_CHUNK:
+                cols = slice((i % 2) * UNIT_COLS, (i % 2 + 1) * UNIT_COLS)
+                nc.scalar.dma_start(
+                    out=out_1.rearrange("b t h d -> (b t) (h d)")[:, cols].rearrange("(m p) n -> p m n", p=P),
+                    in_=result[:, :, cols],
+                )
+            elif (i + 1) * UNIT_HEADS % CHUNK_HEADS == 0:
+                dest = out_0.rearrange("b t h d -> (b t) (h d)")[:, g * CHUNK : (g + 1) * CHUNK]
                 nc.scalar.dma_start(out=dest.rearrange("(m p) n -> p m n", p=P), in_=result[:])
 
         def finish_v(n):

@@ -91,11 +91,11 @@ def tile_llamacausalselfattention_pa_kernel(
         nc.vector.memset(rows_bf[:], 0.0)
         cos_sin = const.tile([P, 2, SEQ_TILES, HEAD // 2], BF16)
         bv_all = const.tile([P, CHUNK], BF16)
+        load_weight_tile(0)
+        load_weight_tile(1)
         load_x(0)
         load_x(1)
-        load_weight_tile(0)
         load_x(2)
-        load_weight_tile(1)
         nc.scalar.dma_start(out=rows_bf[0:Q_HEADS, :], in_=bq.rearrange("(h d) -> h d", d=HEAD))
         nc.scalar.dma_start(
             out=rows_bf[Q_HEADS:ROPE_HEADS, :], in_=bk.rearrange("(h d) -> h d", d=HEAD)
@@ -379,20 +379,26 @@ def tile_llamacausalselfattention_pa_kernel(
         spread_small_vectors()
         for n in unit_heads(0):
             acc_tiles[n] = psum_acc.tile([P, TOKENS], F32, tag="acc", name="acc")
-        for c in range(PASSES):
-            turn_x(c)
-            if c >= 1:
-                for n in unit_heads(0):
-                    one_pass(n, c - 1)
+        def weights_of_pass(c):
             regroup(0, "vector", c * UNIT_COLS, (c + 1) * UNIT_COLS)
             regroup(1, "scalar", c * UNIT_COLS, c * UNIT_COLS + OPENING_SCALAR_COLS)
-            quantise_x(c)
-            quantise_unit(0, c, c + 1)
-        turn_tables()
-        for n in unit_heads(0):
-            one_pass(n, PASSES - 1)
-        for c in range(PASSES):
             regroup(1, "vector", c * UNIT_COLS + OPENING_SCALAR_COLS, (c + 1) * UNIT_COLS)
+            quantise_unit(0, c, c + 1)
+
+        weights_of_pass(0)
+        weights_of_pass(1)
+        for c in range(PASSES):
+            turn_x(c)
+        quantise_x(0)
+        quantise_x(1)
+        weights_of_pass(2)
+        quantise_x(2)
+        weights_of_pass(3)
+        quantise_x(3)
+        turn_tables()
+        for c in range(PASSES):
+            for n in unit_heads(0):
+                one_pass(n, c)
         load_behind(1)
         scale_tables()
         quantise_unit(1)
@@ -422,7 +428,8 @@ def tile_llamacausalselfattention_pa_kernel(
             if prep < UNITS:
                 regroup(prep, "vector", SCALAR_END, UNIT_WORK)
                 load_behind(prep)
-                quantise_unit(prep)
+                quantise_unit(prep, 0, PASSES // 2)
+                quantise_unit(prep, PASSES // 2, PASSES)
         for n in unit_heads(UNITS - 1):
             start_head(n)
         norm_factors(ROPE_UNITS - 1)

@@ -40,6 +40,9 @@ GPSIMD_END = 384
 SCALAR_END = 704
 OPENING_SCALAR_COLS = 192
 ONES_COLS = 64
+WARM_FIRST = 6
+WARM_PACED = 3
+WARM_BETWEEN = 2
 GAIN_COL = ROPE_HEADS
 
 FLOPS = 2 * TOKENS * WIDTH * (Q_HEADS + 2 * KV_HEADS) * HEAD
@@ -124,6 +127,14 @@ def tile_llamacausalselfattention_pa_kernel(
         nc.vector.tensor_copy(out=swap_pairs[:, :, 1], in_=ident_pairs[:, :, 0])
         ones = const.tile([P, ONES_COLS], F32)
         nc.vector.memset(ones[:], 1.0)
+
+        zeros = const.tile([P, CHUNK], BF16)
+        nc.vector.memset(zeros[:], 0.0)
+        unread = psum_ss.tile([P, CHUNK], F32, name="sum_squares")
+
+        def keep_warm(count, moving):
+            for k in range(count):
+                nc.tensor.matmul(out=unread[:], lhsT=zeros[:, 0:P], rhs=moving, start=True, stop=True)
 
         rows_f32 = const.tile([P, P], F32)
         spread = const.tile([P, 2, SEQ_TILES, HEAD], F32)
@@ -385,10 +396,14 @@ def tile_llamacausalselfattention_pa_kernel(
             regroup(1, "vector", c * UNIT_COLS + OPENING_SCALAR_COLS, (c + 1) * UNIT_COLS)
             quantise_unit(0, c, c + 1)
 
+        keep_warm(WARM_FIRST, zeros[:])
+        keep_warm(WARM_PACED, raw_tiles[0][:, 0, :])
+        keep_warm(WARM_PACED, raw_tiles[1][:, 0, :])
         weights_of_pass(0)
         weights_of_pass(1)
         for c in range(PASSES):
             turn_x(c)
+            keep_warm(WARM_BETWEEN, zeros[:])
         quantise_x(0)
         quantise_x(1)
         weights_of_pass(2)

@@ -42,7 +42,6 @@ OPENING_SCALAR_COLS = 192
 ONES_COLS = 64
 WARM_FIRST = 6
 WARM_PACED = 3
-WARM_BETWEEN = 2
 GAIN_COL = ROPE_HEADS
 
 FLOPS = 2 * TOKENS * WIDTH * (Q_HEADS + 2 * KV_HEADS) * HEAD
@@ -90,14 +89,16 @@ def tile_llamacausalselfattention_pa_kernel(
         def load_x(c):
             nc.sync.dma_start(out=x_raw[:, c, :, :], in_=x_blocks[:, :, c * K_PASS : (c + 1) * K_PASS])
 
+        zeros = const.tile([P, CHUNK], BF16)
+        nc.vector.memset(zeros[:], 0.0)
         rows_bf = const.tile([P, P], BF16)
         nc.vector.memset(rows_bf[:], 0.0)
         cos_sin = const.tile([P, 2, SEQ_TILES, HEAD // 2], BF16)
         bv_all = const.tile([P, CHUNK], BF16)
-        load_weight_tile(0)
-        load_weight_tile(1)
         load_x(0)
+        load_weight_tile(0)
         load_x(1)
+        load_weight_tile(1)
         load_x(2)
         nc.scalar.dma_start(out=rows_bf[0:Q_HEADS, :], in_=bq.rearrange("(h d) -> h d", d=HEAD))
         nc.scalar.dma_start(
@@ -106,8 +107,10 @@ def tile_llamacausalselfattention_pa_kernel(
         nc.scalar.dma_start(
             out=rows_bf[GAIN_COL : GAIN_COL + 1, :], in_=qn_w.rearrange("(o d) -> o d", o=1)
         )
+        load_weight_tile(2)
         load_x(3)
-        for j in range(2, RAW_BUFS):
+        load_weight_tile(3)
+        for j in range(PASSES, RAW_BUFS):
             load_weight_tile(j)
         warm = const.tile([P, 2], F32)
         nc.vector.memset(warm[:], 1.0)
@@ -128,8 +131,6 @@ def tile_llamacausalselfattention_pa_kernel(
         ones = const.tile([P, ONES_COLS], F32)
         nc.vector.memset(ones[:], 1.0)
 
-        zeros = const.tile([P, CHUNK], BF16)
-        nc.vector.memset(zeros[:], 0.0)
         unread = psum_ss.tile([P, CHUNK], F32, name="sum_squares")
 
         def keep_warm(count, moving):
@@ -154,9 +155,9 @@ def tile_llamacausalselfattention_pa_kernel(
                 nc.gpsimd.tensor_scalar(out=out, in0=in0, scalar1=factor, scalar2=0.0, op0=ALU.mult, op1=ALU.add)
 
         def turn_tables():
-            rows_ps = psum_acc.tile([P, P], F32, tag="acc")
+            rows_ps = psum_back.tile([P, P], F32, tag="back")
             nc.tensor.transpose(rows_ps[:], rows_f32[:], ident[:])
-            spread_ps = psum_acc.tile([P, 2, SEQ_TILES, P], F32, tag="acc")
+            spread_ps = psum_back.tile([P, 2, SEQ_TILES, P], F32, tag="back")
             for s in range(2):
                 for a in range(SEQ_TILES):
                     nc.tensor.transpose(spread_ps[:, s, a, :], spread[:, s, a, :], ident[:])
@@ -396,24 +397,34 @@ def tile_llamacausalselfattention_pa_kernel(
             regroup(1, "vector", c * UNIT_COLS + OPENING_SCALAR_COLS, (c + 1) * UNIT_COLS)
             quantise_unit(0, c, c + 1)
 
-        keep_warm(WARM_FIRST, zeros[:])
-        keep_warm(WARM_PACED, raw_tiles[0][:, 0, :])
-        keep_warm(WARM_PACED, raw_tiles[1][:, 0, :])
-        weights_of_pass(0)
-        weights_of_pass(1)
-        for c in range(PASSES):
-            turn_x(c)
-            keep_warm(WARM_BETWEEN, zeros[:])
-        quantise_x(0)
-        quantise_x(1)
-        weights_of_pass(2)
-        quantise_x(2)
-        weights_of_pass(3)
-        quantise_x(3)
-        turn_tables()
-        for c in range(PASSES):
+        def passes_of_first_unit(c):
             for n in unit_heads(0):
                 one_pass(n, c)
+
+        def paced(c):
+            keep_warm(WARM_PACED, raw_tiles[c][:, 0, :])
+
+        keep_warm(WARM_FIRST, zeros[:])
+        turn_x(0)
+        paced(0)
+        weights_of_pass(0)
+        quantise_x(0)
+        turn_x(1)
+        paced(1)
+        weights_of_pass(1)
+        quantise_x(1)
+        turn_x(2)
+        passes_of_first_unit(0)
+        paced(2)
+        weights_of_pass(2)
+        quantise_x(2)
+        turn_x(3)
+        passes_of_first_unit(1)
+        weights_of_pass(3)
+        turn_tables()
+        quantise_x(3)
+        passes_of_first_unit(2)
+        passes_of_first_unit(3)
         load_behind(1)
         scale_tables()
         quantise_unit(1)

@@ -25,11 +25,9 @@ SEQ_TILES = SEQ // P
 CHUNK = 512
 CHUNK_HEADS = CHUNK // HEAD
 Q_CHUNKS = Q_HEADS // CHUNK_HEADS
-K_CHUNK = Q_CHUNKS
-V_CHUNK = Q_CHUNKS + 1
 CHUNKS = Q_CHUNKS + 2
 W_TILES = CHUNKS * PASSES
-ROPE_HEADS = Q_HEADS + KV_HEADS
+ROPE_HEADS = KV_HEADS + Q_HEADS
 UNIT_HEADS = 2
 ROPE_UNITS = ROPE_HEADS // UNIT_HEADS
 UNIT_COLS = UNIT_HEADS * HEAD
@@ -70,9 +68,9 @@ def tile_llamacausalselfattention_pa_kernel(
         x_raw = xpool.tile([P, PASSES, TOKEN_TILES, K_PASS], BF16)
 
         def weight_columns(g):
-            if g < Q_CHUNKS:
-                return Wq[:, g * CHUNK : (g + 1) * CHUNK]
-            return Wk if g == K_CHUNK else Wv
+            if g == 0:
+                return Wk
+            return Wv if g > Q_CHUNKS else Wq[:, (g - 1) * CHUNK : g * CHUNK]
 
         raw_tiles = {}
         grouped_tiles = {}
@@ -100,9 +98,9 @@ def tile_llamacausalselfattention_pa_kernel(
         load_x(1)
         load_weight_tile(1)
         load_x(2)
-        nc.scalar.dma_start(out=rows_bf[0:Q_HEADS, :], in_=bq.rearrange("(h d) -> h d", d=HEAD))
+        nc.scalar.dma_start(out=rows_bf[0:KV_HEADS, :], in_=bk.rearrange("(h d) -> h d", d=HEAD))
         nc.scalar.dma_start(
-            out=rows_bf[Q_HEADS:ROPE_HEADS, :], in_=bk.rearrange("(h d) -> h d", d=HEAD)
+            out=rows_bf[KV_HEADS:ROPE_HEADS, :], in_=bq.rearrange("(h d) -> h d", d=HEAD)
         )
         nc.scalar.dma_start(
             out=rows_bf[GAIN_COL : GAIN_COL + 1, :], in_=qn_w.rearrange("(o d) -> o d", o=1)
@@ -166,7 +164,7 @@ def tile_llamacausalselfattention_pa_kernel(
 
         def scale_tables():
             nc.scalar.copy(out=per_feature[:], in_=table_banks["rows"][:])
-            for w in range(2):
+            for w in (1, 0):
                 nc.scalar.activation(
                     out=tables[:, w, :, :],
                     in_=table_banks["spread"][:].rearrange("p s a t -> p s (a t)"),
@@ -291,7 +289,7 @@ def tile_llamacausalselfattention_pa_kernel(
         def rotate_head(n):
             acc = acc_tiles[n]
             bias = per_feature[:, n : n + 1]
-            w = 0 if n < Q_HEADS else 1
+            w = 1 if n < KV_HEADS else 0
             by_cos = work.tile([P, TOKENS], F32)
             by_sin = work.tile([P, TOKENS], F32)
             for s, term in enumerate((by_cos, by_sin)):
@@ -363,14 +361,16 @@ def tile_llamacausalselfattention_pa_kernel(
                         func=ACT.Copy,
                         scale=rstd_tiles[i][:, h, m : m + 1],
                     )
-            if g == K_CHUNK:
+            if g == 0:
+                dest = out_1.rearrange("b t h d -> (b t) (h d)")
+            else:
+                dest = out_0.rearrange("b t h d -> (b t) (h d)")[:, (g - 1) * CHUNK : g * CHUNK]
+            if g == Q_CHUNKS:
                 cols = slice((i % 2) * UNIT_COLS, (i % 2 + 1) * UNIT_COLS)
                 nc.scalar.dma_start(
-                    out=out_1.rearrange("b t h d -> (b t) (h d)")[:, cols].rearrange("(m p) n -> p m n", p=P),
-                    in_=result[:, :, cols],
+                    out=dest[:, cols].rearrange("(m p) n -> p m n", p=P), in_=result[:, :, cols]
                 )
             elif (i + 1) * UNIT_HEADS % CHUNK_HEADS == 0:
-                dest = out_0.rearrange("b t h d -> (b t) (h d)")[:, g * CHUNK : (g + 1) * CHUNK]
                 nc.scalar.dma_start(out=dest.rearrange("(m p) n -> p m n", p=P), in_=result[:])
 
         def finish_v(n):

@@ -389,7 +389,7 @@ def tile_llamacausalselfattention_pa_kernel(
             )
 
         spread_small_vectors()
-        for n in unit_heads(0):
+        for n in range(2 * UNIT_HEADS):
             acc_tiles[n] = psum_acc.tile([P, TOKENS], F32, tag="acc", name="acc")
         def weights_of_pass(c):
             regroup(0, "vector", c * UNIT_COLS, (c + 1) * UNIT_COLS)
@@ -397,8 +397,8 @@ def tile_llamacausalselfattention_pa_kernel(
             regroup(1, "vector", c * UNIT_COLS + OPENING_SCALAR_COLS, (c + 1) * UNIT_COLS)
             quantise_unit(0, c, c + 1)
 
-        def passes_of_first_unit(c):
-            for n in unit_heads(0):
+        def passes_of_unit(u, c):
+            for n in unit_heads(u):
                 one_pass(n, c)
 
         def paced(c):
@@ -412,22 +412,27 @@ def tile_llamacausalselfattention_pa_kernel(
         turn_x(1)
         paced(1)
         weights_of_pass(1)
+        quantise_unit(1, 0, 1)
         quantise_x(1)
         turn_x(2)
-        passes_of_first_unit(0)
+        passes_of_unit(0, 0)
         paced(2)
         weights_of_pass(2)
+        quantise_unit(1, 1, 2)
         quantise_x(2)
         turn_x(3)
-        passes_of_first_unit(1)
+        passes_of_unit(0, 1)
+        passes_of_unit(1, 0)
         weights_of_pass(3)
         turn_tables()
         quantise_x(3)
-        passes_of_first_unit(2)
-        passes_of_first_unit(3)
+        passes_of_unit(0, 2)
+        passes_of_unit(0, 3)
         load_behind(1)
         scale_tables()
-        quantise_unit(1)
+        quantise_unit(1, 2, PASSES)
+        for c in range(1, PASSES):
+            passes_of_unit(1, c)
         for n in unit_heads(0):
             square_head(n)
         for i in range(ROPE_UNITS):
@@ -436,13 +441,14 @@ def tile_llamacausalselfattention_pa_kernel(
             if prep < UNITS:
                 regroup(prep, "gpsimd", 0, GPSIMD_END)
                 regroup(prep, "scalar", GPSIMD_END, SCALAR_END)
-            start_head(first + UNIT_HEADS)
             if i >= 1:
+                start_head(first + UNIT_HEADS)
                 norm_factors(i - 1)
                 finish(i - 1)
             if i == 2:
                 nc.scalar.dma_start(out=bv_all[:], in_=bv.partition_broadcast(P))
-            start_head(second + UNIT_HEADS)
+            if i >= 1:
+                start_head(second + UNIT_HEADS)
             rotate_head(first)
             rotate_head(second)
             turn_back_head(first)

from contextlib import ExitStack

import concourse.mybir as mybir
from concourse.masks import make_identity

F32 = mybir.dt.float32
BF16 = mybir.dt.bfloat16
U32 = mybir.dt.uint32
U8 = mybir.dt.uint8
FP8X4 = mybir.dt.float8_e4m3fn_x4
ALU = mybir.AluOpType
ACT = mybir.ActivationFunctionType

BATCH, SEQ, WIDTH = 2, 256, 2048
Q_HEADS, KV_HEADS, HEAD = 16, 4, 128
EPS = 1e-5

P = 128
PACK = 4
K_PASS = P * PACK
PASSES = WIDTH // K_PASS
TOKENS = BATCH * SEQ
TOKEN_TILES = TOKENS // P
SEQ_TILES = SEQ // P
CHUNK = 512
CHUNK_HEADS = CHUNK // HEAD
Q_CHUNKS = Q_HEADS // CHUNK_HEADS
CHUNKS = Q_CHUNKS + 2
W_TILES = CHUNKS * PASSES
ROPE_HEADS = KV_HEADS + Q_HEADS
UNIT_HEADS = 2
ROPE_UNITS = ROPE_HEADS // UNIT_HEADS
UNIT_COLS = UNIT_HEADS * HEAD
UNITS = CHUNKS * CHUNK // UNIT_COLS
RAW_BUFS = 8
UNIT_WORK = PASSES * UNIT_COLS
GPSIMD_END = 384
SCALAR_END = 704
OPENING_SCALAR_COLS = 192
ONES_COLS = 64
WARM_FIRST = 6
WARM_PACED = 3
GAIN_COL = ROPE_HEADS

FLOPS = 2 * TOKENS * WIDTH * (Q_HEADS + 2 * KV_HEADS) * HEAD


def tile_llamacausalselfattention_pa_kernel(
    tc, x, Wq, bq, Wk, bk, Wv, bv, qn_w, kn_w, freqs_cos, freqs_sin, out_0, out_1, out_2
):
    nc = tc.nc
    with ExitStack() as pools:
        const = pools.enter_context(tc.tile_pool(name="const", bufs=1))
        xpool = pools.enter_context(tc.tile_pool(name="xpool", bufs=1))
        wraw = pools.enter_context(tc.tile_pool(name="wraw", bufs=RAW_BUFS))
        wgrp = pools.enter_context(tc.tile_pool(name="wgrp", bufs=1))
        wmx = pools.enter_context(tc.tile_pool(name="wmx", bufs=1))
        work = pools.enter_context(tc.tile_pool(name="work", bufs=4))
        stats = pools.enter_context(tc.tile_pool(name="stats", bufs=4))
        outs = pools.enter_context(tc.tile_pool(name="outs", bufs=3))
        vout = pools.enter_context(tc.tile_pool(name="vout", bufs=4))
        psum_acc = pools.enter_context(tc.psum_pool(name="psum_acc", bufs=4))
        psum_back = pools.enter_context(tc.psum_pool(name="psum_back", bufs=3))
        psum_ss = pools.enter_context(tc.psum_pool(name="psum_ss", bufs=1))
        pools.enter_context(tc.manual_schedule())

        x_blocks = x.flatten_outer_dims().rearrange("(m p) k -> p m k", p=P)
        x_raw = xpool.tile([P, PASSES, TOKEN_TILES, K_PASS], BF16)

        def weight_columns(g):
            if g == 0:
                return Wk
            return Wv if g > Q_CHUNKS else Wq[:, (g - 1) * CHUNK : g * CHUNK]

        raw_tiles = {}
        grouped_tiles = {}

        def load_weight_tile(j):
            g, c = divmod(j, PASSES)
            raw = wraw.tile([P, PACK, CHUNK], BF16)
            nc.sync.dma_start(
                out=raw[:],
                in_=weight_columns(g).rearrange("(c p t) n -> c p t n", p=P, t=PACK)[c],
            )
            raw_tiles[j] = raw

        def load_x(c):
            nc.sync.dma_start(out=x_raw[:, c, :, :], in_=x_blocks[:, :, c * K_PASS : (c + 1) * K_PASS])

        zeros = const.tile([P, CHUNK], BF16)
        nc.vector.memset(zeros[:], 0.0)
        rows_bf = const.tile([P, P], BF16)
        nc.vector.memset(rows_bf[:], 0.0)
        cos_sin = const.tile([P, 2, SEQ_TILES, HEAD // 2], BF16)
        bv_all = const.tile([P, CHUNK], BF16)
        load_x(0)
        load_weight_tile(0)
        load_x(1)
        load_weight_tile(1)
        load_x(2)
        nc.scalar.dma_start(out=rows_bf[0:KV_HEADS, :], in_=bk.rearrange("(h d) -> h d", d=HEAD))
        nc.scalar.dma_start(
            out=rows_bf[KV_HEADS:ROPE_HEADS, :], in_=bq.rearrange("(h d) -> h d", d=HEAD)
        )
        nc.scalar.dma_start(
            out=rows_bf[GAIN_COL : GAIN_COL + 1, :], in_=qn_w.rearrange("(o d) -> o d", o=1)
        )
        load_weight_tile(2)
        load_x(3)
        load_weight_tile(3)
        for j in range(PASSES, RAW_BUFS):
            load_weight_tile(j)
        warm = const.tile([P, 2], F32)
        nc.vector.memset(warm[:], 1.0)
        nc.scalar.activation(out=warm[:, 1:2], in_=warm[:, 0:1], func=ACT.Abs_reciprocal_sqrt)

        ident = const.tile([P, P], F32)
        make_identity(nc, ident[:])
        nc.gpsimd.dma_start(
            out=rows_bf[GAIN_COL + 1 : GAIN_COL + 2, :], in_=kn_w.rearrange("(o d) -> o d", o=1)
        )
        nc.gpsimd.dma_start(out=cos_sin[:, 0, :, :], in_=freqs_cos.rearrange("(a p) j -> p a j", p=P))
        nc.gpsimd.dma_start(out=cos_sin[:, 1, :, :], in_=freqs_sin.rearrange("(a p) j -> p a j", p=P))
        swap = const.tile([P, P], F32)
        ident_pairs = ident[:].rearrange("p (j two) -> p j two", two=2)
        swap_pairs = swap[:].rearrange("p (j two) -> p j two", two=2)
        nc.vector.tensor_copy(out=swap_pairs[:, :, 0], in_=ident_pairs[:, :, 1])
        nc.vector.tensor_copy(out=swap_pairs[:, :, 1], in_=ident_pairs[:, :, 0])
        ones = const.tile([P, ONES_COLS], F32)
        nc.vector.memset(ones[:], 1.0)

        unread = psum_ss.tile([P, CHUNK], F32, name="sum_squares")

        def keep_warm(count, moving):
            for k in range(count):
                nc.tensor.matmul(out=unread[:], lhsT=zeros[:, 0:P], rhs=moving, start=True, stop=True)

        rows_f32 = const.tile([P, P], F32)
        spread = const.tile([P, 2, SEQ_TILES, HEAD], F32)
        per_feature = const.tile([P, P], F32)
        tables = const.tile([P, 2, 2, SEQ], F32)
        table_banks = {}

        def spread_small_vectors():
            cos_pairs = spread[:, 0, :, :].rearrange("p a (j two) -> p a j two", two=2)
            sin_pairs = spread[:, 1, :, :].rearrange("p a (j two) -> p a j two", two=2)
            for out, in0, factor in (
                (rows_f32[:], rows_bf[:], 1.0),
                (cos_pairs, cos_sin[:, 0, :, :].unsqueeze(3).to_broadcast([P, SEQ_TILES, HEAD // 2, 2]), 1.0),
                (sin_pairs[:, :, :, 0], cos_sin[:, 1, :, :], 1.0),
                (sin_pairs[:, :, :, 1], cos_sin[:, 1, :, :], -1.0),
            ):
                nc.gpsimd.tensor_scalar(out=out, in0=in0, scalar1=factor, scalar2=0.0, op0=ALU.mult, op1=ALU.add)

        def turn_tables():
            rows_ps = psum_back.tile([P, P], F32, tag="back")
            nc.tensor.transpose(rows_ps[:], rows_f32[:], ident[:])
            spread_ps = psum_back.tile([P, 2, SEQ_TILES, P], F32, tag="back")
            for s in range(2):
                for a in range(SEQ_TILES):
                    nc.tensor.transpose(spread_ps[:, s, a, :], spread[:, s, a, :], ident[:])
            table_banks["rows"] = rows_ps
            table_banks["spread"] = spread_ps

        def scale_tables():
            nc.scalar.copy(out=per_feature[:], in_=table_banks["rows"][:])
            for w in (1, 0):
                nc.scalar.activation(
                    out=tables[:, w, :, :],
                    in_=table_banks["spread"][:].rearrange("p s a t -> p s (a t)"),
                    func=ACT.Copy,
                    scale=per_feature[:, GAIN_COL + w : GAIN_COL + w + 1],
                )

        x_grouped = xpool.tile([P, PASSES, TOKENS * PACK], BF16, align_bytes=64)
        x_codes = xpool.tile([P, PASSES, TOKENS], U32, align_bytes=64)
        x_scales = xpool.tile([P, PASSES, TOKENS], U8, align_bytes=64)
        x_grouped_words = x_grouped[:].bitcast(F32).rearrange("p c (m r u) -> p c m r u", m=TOKEN_TILES, u=2)

        def quantise_x(c):
            nc.vector.quantize_mx(
                out=x_codes[:, c, :].bitcast(FP8X4), scales=x_scales[:, c, :], in_=x_grouped[:, c, :]
            )

        def turn_x(c):
            x_words = x_raw[:, c, :, :].bitcast(F32).rearrange("p m (w u) -> p m u w", u=2)
            for half in range(2):
                turned = psum_back.tile([P, 2, 2, P], F32, tag="back")
                for m2 in range(2):
                    for u in range(2):
                        nc.tensor.transpose(turned[:, m2, u, :], x_words[:, 2 * half + m2, u, :], ident[:])
                nc.scalar.copy(
                    out=x_grouped_words[:, c, 2 * half : 2 * half + 2, :, :],
                    in_=turned[:].rearrange("p m u r -> p m r u"),
                )

        w_codes = [wmx.tile([P, PASSES, UNIT_COLS], U32, align_bytes=64, name="w_codes%d" % u) for u in range(UNITS)]
        w_scales = [wmx.tile([P, PASSES, UNIT_COLS], U8, align_bytes=64, name="w_scales%d" % u) for u in range(UNITS)]

        def grouped_of(u):
            if u not in grouped_tiles:
                grouped_tiles[u] = wgrp.tile(
                    [P, PASSES, UNIT_COLS, PACK], BF16, align_bytes=64, name="grouped_first" if u == 0 else "grouped"
                )
            return grouped_tiles[u]

        def regroup(u, engine, lo, hi):
            g, half = divmod(u, CHUNK // UNIT_COLS)
            for c in range(PASSES):
                a = max(lo, c * UNIT_COLS) - c * UNIT_COLS
                b = min(hi, (c + 1) * UNIT_COLS) - c * UNIT_COLS
                if a >= b:
                    continue
                dst = grouped_of(u)[:, c, a:b, :].rearrange("p (n i) t -> p n t i", i=4)
                src = raw_tiles[g * PASSES + c][:, :, half * UNIT_COLS + a : half * UNIT_COLS + b].rearrange(
                    "p t (n i) -> p n t i", i=4
                )
                if engine == "vector":
                    nc.vector.tensor_copy(out=dst, in_=src)
                elif engine == "scalar":
                    nc.scalar.copy(out=dst, in_=src)
                else:
                    nc.gpsimd.tensor_scalar(out=dst, in0=src, scalar1=1.0, scalar2=0.0, op0=ALU.mult, op1=ALU.add)

        def load_behind(u):
            g, half = divmod(u, CHUNK // UNIT_COLS)
            if half == 1 and g + 2 < CHUNKS:
                for c in range(PASSES):
                    load_weight_tile((g + 2) * PASSES + c)

        def quantise_unit(u, first_pass=0, last_pass=PASSES):
            nc.vector.quantize_mx(
                out=w_codes[u][:, first_pass:last_pass, :].rearrange("p c n -> p (c n)").bitcast(FP8X4),
                scales=w_scales[u][:, first_pass:last_pass, :].rearrange("p c n -> p (c n)"),
                in_=grouped_of(u)[:, first_pass:last_pass, :, :].rearrange("p c n t -> p (c n t)"),
            )

        acc_tiles = {}
        rotated = {}
        squared = {}
        back_tiles = {}
        rstd_tiles = {}
        out_tiles = {}
        sums_tiles = {}

        def unit_heads(i):
            return range(i * UNIT_HEADS, (i + 1) * UNIT_HEADS)

        def one_pass(n, c):
            u, h = divmod(n, UNIT_HEADS)
            cols = slice(h * HEAD, (h + 1) * HEAD)
            nc.tensor.matmul_mx(
                out=acc_tiles[n][:],
                lhsT=w_codes[u][:, c, cols].bitcast(FP8X4),
                lhsT_scale=w_scales[u][:, c, cols],
                rhs=x_codes[:, c, :].bitcast(FP8X4),
                rhs_scale=x_scales[:, c, :],
                start=(c == 0),
                stop=(c == PASSES - 1),
            )

        def project_head(n):
            acc_tiles[n] = psum_acc.tile([P, TOKENS], F32, tag="acc", name="acc")
            for c in range(PASSES):
                one_pass(n, c)

        def project_v(n):
            u, h = divmod(n, UNIT_HEADS)
            acc_tiles[n] = psum_acc.tile([P, 2, UNIT_COLS], F32, tag="acc", name="acc")
            for mm in range(2):
                tokens = slice((2 * h + mm) * P, (2 * h + mm + 1) * P)
                for c in range(PASSES):
                    nc.tensor.matmul_mx(
                        out=acc_tiles[n][:, mm, :],
                        lhsT=x_codes[:, c, tokens].bitcast(FP8X4),
                        lhsT_scale=x_scales[:, c, tokens],
                        rhs=w_codes[u][:, c, :].bitcast(FP8X4),
                        rhs_scale=w_scales[u][:, c, :],
                        start=(c == 0),
                        stop=(c == PASSES - 1),
                    )

        def start_head(n):
            if n < ROPE_HEADS:
                project_head(n)
            else:
                project_v(n)

        def rotate_head(n):
            acc = acc_tiles[n]
            bias = per_feature[:, n : n + 1]
            w = 1 if n < KV_HEADS else 0
            by_cos = work.tile([P, TOKENS], F32)
            by_sin = work.tile([P, TOKENS], F32)
            for s, term in enumerate((by_cos, by_sin)):
                nc.vector.scalar_tensor_tensor(
                    out=term[:].rearrange("p (b t) -> p b t", b=BATCH),
                    in0=acc[:].rearrange("p (b t) -> p b t", b=BATCH),
                    scalar=bias,
                    in1=tables[:, w, s, :].unsqueeze(1).to_broadcast([P, BATCH, SEQ]),
                    op0=ALU.add,
                    op1=ALU.mult,
                )
            rotated[n] = (by_cos, by_sin)

        def square_head(n):
            squares = work.tile([P, TOKENS], F32)
            nc.scalar.activation(
                out=squares[:], in_=acc_tiles[n][:], func=ACT.Square, bias=per_feature[:, n : n + 1], scale=1.0
            )
            squared[n] = squares

        def turn_back_head(n):
            i, h = divmod(n, UNIT_HEADS)
            if i not in sums_tiles:
                sums_tiles[i] = psum_ss.tile([P, UNIT_HEADS, TOKEN_TILES, ONES_COLS], F32, name="sum_squares")
            by_cos, by_sin = rotated[n]
            back = psum_back.tile([P, TOKEN_TILES, HEAD], F32, tag="back")

            def sum_tile(m):
                nc.tensor.matmul(
                    out=sums_tiles[i][:, h, m, :], lhsT=squared[n][:, m * P : (m + 1) * P], rhs=ones[:],
                    start=True, stop=True,
                )

            for m in range(TOKEN_TILES):
                tokens = slice(m * P, (m + 1) * P)
                if h == 0:
                    sum_tile(m)
                nc.tensor.matmul(
                    out=back[:, m, :], lhsT=by_cos[:, tokens], rhs=ident[:],
                    is_transpose=True, start=True, stop=False,
                )
                nc.tensor.matmul(
                    out=back[:, m, :], lhsT=by_sin[:, tokens], rhs=swap[:],
                    is_transpose=True, start=False, stop=True,
                )
                if h == 1:
                    sum_tile(m)
            back_tiles[n] = back

        def norm_factors(i):
            rstd = stats.tile([P, UNIT_HEADS, TOKEN_TILES], F32)
            nc.scalar.activation(
                out=rstd[:], in_=sums_tiles[i][:, :, :, 0],
                func=ACT.Abs_reciprocal_sqrt, bias=EPS, scale=1.0 / HEAD,
            )
            rstd_tiles[i] = rstd

        def finish(i):
            g = (i * UNIT_HEADS) // CHUNK_HEADS
            if g not in out_tiles:
                out_tiles[g] = outs.tile([P, TOKEN_TILES, CHUNK], F32, name="result")
            result = out_tiles[g]
            for h, n in enumerate(unit_heads(i)):
                local = n % CHUNK_HEADS
                for m in range(TOKEN_TILES):
                    nc.scalar.activation(
                        out=result[:, m, local * HEAD : (local + 1) * HEAD],
                        in_=back_tiles[n][:, m, :],
                        func=ACT.Copy,
                        scale=rstd_tiles[i][:, h, m : m + 1],
                    )
            if g == 0:
                dest = out_1.rearrange("b t h d -> (b t) (h d)")
            else:
                dest = out_0.rearrange("b t h d -> (b t) (h d)")[:, (g - 1) * CHUNK : g * CHUNK]
            if g == Q_CHUNKS:
                cols = slice((i % 2) * UNIT_COLS, (i % 2 + 1) * UNIT_COLS)
                nc.scalar.dma_start(
                    out=dest[:, cols].rearrange("(m p) n -> p m n", p=P), in_=result[:, :, cols]
                )
            elif (i + 1) * UNIT_HEADS % CHUNK_HEADS == 0:
                nc.scalar.dma_start(out=dest.rearrange("(m p) n -> p m n", p=P), in_=result[:])

        def finish_v(n):
            u, h = divmod(n, UNIT_HEADS)
            cols = slice((u - ROPE_UNITS) * UNIT_COLS, (u - ROPE_UNITS + 1) * UNIT_COLS)
            v_rows = vout.tile([P, 2, UNIT_COLS], F32)
            nc.vector.tensor_tensor(
                out=v_rows[:], in0=acc_tiles[n][:],
                in1=bv_all[:, cols].unsqueeze(1).to_broadcast([P, 2, UNIT_COLS]), op=ALU.add,
            )
            nc.sync.dma_start(
                out=out_2.rearrange("b t h d -> (b t) (h d)")[2 * h * P : (2 * h + 2) * P, cols].rearrange(
                    "(m p) n -> p m n", p=P
                ),
                in_=v_rows[:],
            )

        spread_small_vectors()
        for n in range(2 * UNIT_HEADS):
            acc_tiles[n] = psum_acc.tile([P, TOKENS], F32, tag="acc", name="acc")
        def weights_of_pass(c):
            regroup(0, "vector", c * UNIT_COLS, (c + 1) * UNIT_COLS)
            regroup(1, "scalar", c * UNIT_COLS, c * UNIT_COLS + OPENING_SCALAR_COLS)
            regroup(1, "vector", c * UNIT_COLS + OPENING_SCALAR_COLS, (c + 1) * UNIT_COLS)
            quantise_unit(0, c, c + 1)

        def passes_of_unit(u, c):
            for n in unit_heads(u):
                one_pass(n, c)

        def paced(c):
            keep_warm(WARM_PACED, raw_tiles[c][:, 0, :])

        keep_warm(WARM_FIRST, zeros[:])
        turn_x(0)
        paced(0)
        weights_of_pass(0)
        quantise_x(0)
        turn_x(1)
        paced(1)
        weights_of_pass(1)
        quantise_unit(1, 0, 1)
        quantise_x(1)
        turn_x(2)
        passes_of_unit(0, 0)
        paced(2)
        weights_of_pass(2)
        quantise_unit(1, 1, 2)
        quantise_x(2)
        turn_x(3)
        passes_of_unit(0, 1)
        passes_of_unit(1, 0)
        weights_of_pass(3)
        turn_tables()
        quantise_x(3)
        passes_of_unit(0, 2)
        passes_of_unit(0, 3)
        load_behind(1)
        scale_tables()
        quantise_unit(1, 2, PASSES)
        for c in range(1, PASSES):
            passes_of_unit(1, c)
        for n in unit_heads(0):
            square_head(n)
        for i in range(ROPE_UNITS):
            first, second = unit_heads(i)
            prep = i + 2
            if prep < UNITS:
                regroup(prep, "gpsimd", 0, GPSIMD_END)
                regroup(prep, "scalar", GPSIMD_END, SCALAR_END)
            if i >= 1:
                start_head(first + UNIT_HEADS)
                norm_factors(i - 1)
                finish(i - 1)
            if i == 2:
                nc.scalar.dma_start(out=bv_all[:], in_=bv.partition_broadcast(P))
            if i >= 1:
                start_head(second + UNIT_HEADS)
            rotate_head(first)
            rotate_head(second)
            turn_back_head(first)
            if i + 1 < ROPE_UNITS:
                square_head(first + UNIT_HEADS)
            turn_back_head(second)
            if i + 1 < ROPE_UNITS:
                square_head(second + UNIT_HEADS)
            if prep < UNITS:
                regroup(prep, "vector", SCALAR_END, UNIT_WORK)
                load_behind(prep)
                quantise_unit(prep, 0, PASSES // 2)
                quantise_unit(prep, PASSES // 2, PASSES)
        for n in unit_heads(UNITS - 1):
            start_head(n)
        norm_factors(ROPE_UNITS - 1)
        finish(ROPE_UNITS - 1)
        for u in range(ROPE_UNITS, UNITS):
            for n in unit_heads(u):
                finish_v(n)
